import numpy as np
import ml_dtypes


def mxq(x, axis, fmt="e4m3"):
    dtype, down = {"e4m3": (ml_dtypes.float8_e4m3fn, 7), "e5m2": (ml_dtypes.float8_e5m2, 14)}[fmt]
    v = np.moveaxis(np.asarray(x, np.float32).astype(ml_dtypes.bfloat16).astype(np.float64), axis, -1)
    blocks = v.reshape(v.shape[:-1] + (-1, 32))
    amax = np.abs(blocks).max(-1, keepdims=True)
    byte = np.maximum(np.where(amax > 0, np.frexp(amax)[1] - 1 + 127, 0) - down, 1)
    scale = np.exp2(byte - 127.0)
    codes = (blocks / scale).astype(np.float32).astype(dtype).astype(np.float64)
    return np.moveaxis((codes * scale).reshape(v.shape), -1, axis)


WIDE = False


def mx_kscale(k):
    if not WIDE:
        return np.ones(k)
    levels = np.array([10, -10, 5, -5, 0])
    a = np.random.permutation(np.resize(levels, k // 512 * 4)).reshape(k // 512, 4)
    idx = np.arange(k)
    return np.exp2(a[idx // 512, idx % 128 // 32])


BF16 = ml_dtypes.bfloat16


def bf(x):
    return np.asarray(x, np.float32).astype(BF16)


def f64(x):
    return np.asarray(x).astype(np.float64)


B, R, C0, C1, C2, H0, H1, H2 = 16, 128, 1024, 2048, 2048, 16, 8, 8
EPS = 1e-12
MU = 0.5
P = H0 // H1
N0, N1 = H0 * H0, H1 * H1


def setup_inputs():
    s0, s1 = mx_kscale(C0), mx_kscale(C1)
    return {"fmap_low": bf((np.random.standard_normal((B, C0, H0, H0)) + MU) * s0[None, :, None, None]),
            "w_low": bf(np.random.standard_normal((R, C0)) / np.sqrt(C0) / s0[None, :]),
            "fmap_high": bf((np.random.standard_normal((B, C1, H1, H1)) + MU) * s1[None, :, None, None]),
            "w_high": bf(np.random.standard_normal((R, C1)) / np.sqrt(C1) / s1[None, :])}


def cam(fmap, w, c, n):
    return mxq(f64(w), 1, "e4m3") @ mxq(f64(fmap).reshape(B, c, n), 1, "e4m3")


def unit(v):
    return v / np.maximum(np.sqrt((v * v).sum(-1, keepdims=True)), EPS)


def reference(fmap_low, w_low, fmap_high, w_high):
    low = cam(fmap_low, w_low, C0, N0)
    high = cam(fmap_high, w_high, C1, N1)
    low = low.reshape(B, R, H1, P, H1, P).mean(axis=(3, 5)).reshape(B, R, N1)
    lo = unit(low).transpose(1, 0, 2).reshape(R, B * N1)
    hi = unit(high).transpose(1, 0, 2).reshape(R, B * N1)
    return (mxq(lo, 1, "e4m3") @ mxq(hi, 1, "e4m3").T) / B

@@ -1,0 +1,226 @@
+from contextlib import ExitStack
+
+import concourse.mybir as mybir
+from concourse.masks import make_identity
+
+BF16 = mybir.dt.bfloat16
+F32 = mybir.dt.float32
+U32 = mybir.dt.uint32
+U8 = mybir.dt.uint8
+FP8X4 = mybir.dt.float8_e4m3fn_x4
+ACT = mybir.ActivationFunctionType
+ALU = mybir.AluOpType
+
+P = 128
+PACK = 4
+K_PASS = P * PACK
+
+SAMPLES = 16
+NODES = 128
+C_LOW, C_HIGH = 1024, 2048
+LOW_PASSES, HIGH_PASSES = C_LOW // K_PASS, C_HIGH // K_PASS
+SIDE = 8
+WINDOW = 2
+POSITIONS = SIDE * SIDE
+EPS = 1e-12
+
+PAIR = 2
+PAIR_COLUMNS = PAIR * POSITIONS
+SLABS = 4
+CHUNK = SLABS * PAIR_COLUMNS * PACK
+HALVES = SAMPLES * POSITIONS // K_PASS
+HALF_SAMPLES = SAMPLES // HALVES
+HALF_PAIRS = HALF_SAMPLES // PAIR
+
+FLOPS = 2 * NODES * SAMPLES * (C_LOW * POSITIONS * WINDOW * WINDOW + C_HIGH * POSITIONS + NODES * POSITIONS)
+
+
+def tile_avsl_graph_pa_t_kernel(tc, fmap_low, w_low, fmap_high, w_high, out):
+    nc = tc.nc
+    with ExitStack() as stack:
+        keep = stack.enter_context(tc.tile_pool(name="keep", bufs=1))
+        raws = stack.enter_context(tc.tile_pool(name="raws", bufs=(LOW_PASSES + 1) * SAMPLES // PAIR))
+        stage = stack.enter_context(tc.tile_pool(name="stage", bufs=4))
+        quant = stack.enter_context(tc.tile_pool(name="quant", bufs=8))
+        cams = stack.enter_context(tc.psum_pool(name="cams", bufs=2 * HALVES))
+        turns = stack.enter_context(tc.psum_pool(name="turns", bufs=3))
+        links = stack.enter_context(tc.psum_pool(name="links", bufs=1))
+
+        ident_words = keep.tile([P, P], F32)
+        make_identity(nc, ident_words[:])
+        ident_bf16 = keep.tile([P, P], BF16)
+        make_identity(nc, ident_bf16[:])
+
+        one = keep.tile([P, 1], F32)
+        nc.vector.memset(one[:], 1.0)
+        root_of_one = keep.tile([P, 1], F32)
+        nc.scalar.sqrt(root_of_one[:], one[:])
+
+        w_low_rows = keep.tile([NODES, C_LOW], BF16)
+        nc.sync.dma_start(out=w_low_rows[:], in_=w_low)
+        raw_low = {}
+        for pair in range(SAMPLES // PAIR):
+            for s in range(LOW_PASSES):
+                raw = raws.tile([P, CHUNK], BF16, name="raw_low_%d_%d" % (pair, s), tag="raw")
+                nc.sync.dma_start(
+                    out=raw[:].rearrange("p (b e) -> p b e", b=PAIR),
+                    in_=fmap_low[PAIR * pair : PAIR * (pair + 1), K_PASS * s : K_PASS * (s + 1)].rearrange(
+                        "b (p j) y x -> p b (j y x)", j=PACK
+                    ),
+                )
+                raw_low[(pair, s)] = raw
+        w_high_rows = keep.tile([NODES, C_HIGH], BF16)
+        nc.sync.dma_start(out=w_high_rows[:], in_=w_high)
+        raw_high = {}
+        for pair in range(SAMPLES // PAIR):
+            raw = raws.tile([P, CHUNK], BF16, name="raw_high_%d" % pair, tag="raw")
+            nc.sync.dma_start(
+                out=raw[:].rearrange("p (b s e) -> p b s e", b=PAIR, s=HIGH_PASSES),
+                in_=fmap_high[PAIR * pair : PAIR * (pair + 1)].rearrange(
+                    "b (s p j) y x -> p b s (j y x)", s=HIGH_PASSES, j=PACK
+                ),
+            )
+            raw_high[pair] = raw
+
+        def quantise_weights(rows, passes, level):
+            words = rows[:].bitcast(F32)
+            pass_words = K_PASS // 2
+            grouped = keep.tile([P, passes * NODES * PACK], BF16, name="w_grouped_%s" % level, align_bytes=64)
+            grouped_words = grouped[:].bitcast(F32).rearrange("p (s r u) -> p s r u", r=NODES, u=2)
+            for first in range(0, passes, 2):
+                turned = turns.tile([P, 2, 2, NODES], F32, name="w_turned_%s" % level, tag="turn")
+                for s in range(2):
+                    for u in range(2):
+                        start = pass_words * (first + s)
+                        nc.tensor.transpose(
+                            turned[:, s, u, :], words[:, start + u : start + pass_words : 2], ident_words[:]
+                        )
+                nc.vector.tensor_copy(
+                    out=grouped_words[:, first : first + 2], in_=turned[:].rearrange("p s u r -> p s r u")
+                )
+            codes = keep.tile([P, passes, NODES], U32, name="w_codes_%s" % level, align_bytes=64)
+            scales = keep.tile([P, passes, NODES], U8, name="w_scales_%s" % level, align_bytes=64)
+            nc.vector.quantize_mx(
+                out=codes[:].rearrange("p s r -> p (s r)").bitcast(FP8X4),
+                scales=scales[:].rearrange("p s r -> p (s r)"),
+                in_=grouped[:],
+            )
+            return codes, scales
+
+        def regroup_low(raw):
+            grouped = stage.tile([P, CHUNK], BF16, align_bytes=64)
+            source = raw[:].rearrange(
+                "p (b j yy py xx px) -> p b px yy py xx j", b=PAIR, j=PACK, yy=SIDE, py=WINDOW, xx=SIDE, px=WINDOW
+            )
+            target = grouped[:].rearrange(
+                "p (py px b yy xx j) -> p b px yy py xx j", py=WINDOW, px=WINDOW, b=PAIR, yy=SIDE, xx=SIDE, j=PACK
+            )
+            nc.vector.tensor_copy(out=target[:, 0], in_=source[:, 0])
+            nc.scalar.copy(out=target[:, 1], in_=source[:, 1])
+            return grouped
+
+        def regroup_high(raw):
+            grouped = stage.tile([P, CHUNK], BF16, align_bytes=64)
+            source = raw[:].rearrange("p (b s j i) -> p b s i j", b=PAIR, s=HIGH_PASSES, j=PACK)
+            target = grouped[:].rearrange("p (s b i j) -> p b s i j", s=HIGH_PASSES, b=PAIR, j=PACK)
+            nc.vector.tensor_copy(out=target[:, 0], in_=source[:, 0])
+            nc.scalar.copy(out=target[:, 1], in_=source[:, 1])
+            return grouped
+
+        def add_chunk(acc, grouped, weights, pass_of_slab, opens, closes):
+            w_codes, w_scales = weights
+            codes = quant.tile([P, SLABS, PAIR_COLUMNS], U32, align_bytes=64)
+            scales = quant.tile([P, SLABS, PAIR_COLUMNS], U8, align_bytes=64)
+            nc.vector.quantize_mx(
+                out=codes[:].rearrange("p m c -> p (m c)").bitcast(FP8X4),
+                scales=scales[:].rearrange("p m c -> p (m c)"),
+                in_=grouped[:],
+            )
+            for slab in range(SLABS):
+                s = pass_of_slab[slab]
+                nc.tensor.matmul_mx(
+                    out=acc,
+                    lhsT=w_codes[:, s, :].bitcast(FP8X4),
+                    lhsT_scale=w_scales[:, s, :],
+                    rhs=codes[:, slab, :].bitcast(FP8X4),
+                    rhs_scale=scales[:, slab, :],
+                    start=(opens and slab == 0),
+                    stop=(closes and slab == SLABS - 1),
+                )
+
+        def add_square_sums(sumsq, squares, cam, pair):
+            for b in range(PAIR * pair, PAIR * (pair + 1)):
+                nc.scalar.activation(
+                    out=squares[:, b, :],
+                    in_=cam[:, POSITIONS * b : POSITIONS * (b + 1)],
+                    func=ACT.Square,
+                    accum_out=sumsq[:, b : b + 1],
+                )
+
+        def quantise_unit_rows(cam, sumsq, floor, label):
+            floored = stage.tile([P, HALF_SAMPLES], F32)
+            nc.vector.tensor_scalar_max(out=floored[:], in0=sumsq[:], scalar1=floor * floor)
+            norm = stage.tile([P, HALF_SAMPLES], F32)
+            nc.scalar.sqrt(norm[:], floored[:])
+            inverse = stage.tile([P, HALF_SAMPLES], F32)
+            nc.vector.reciprocal(inverse[:], norm[:])
+            unit = stage.tile([P, K_PASS], BF16)
+            nc.vector.tensor_tensor(
+                out=unit[:].rearrange("p (b i) -> p b i", i=POSITIONS),
+                in0=cam[:].rearrange("p (b i) -> p b i", i=POSITIONS),
+                in1=inverse[:].unsqueeze(2).to_broadcast([P, HALF_SAMPLES, POSITIONS]),
+                op=ALU.mult,
+            )
+            turned = turns.tile([P, PACK, NODES], BF16, tag="turn")
+            for t in range(PACK):
+                nc.tensor.transpose(turned[:, t, :], unit[:, P * t : P * (t + 1)], ident_bf16[:])
+            unit_grouped = stage.tile([P, NODES, PACK], BF16, align_bytes=64)
+            nc.scalar.copy(out=unit_grouped[:], in_=turned[:].rearrange("p t r -> p r t"))
+            codes = keep.tile([P, NODES], U32, name="unit_codes_%s" % label, align_bytes=64)
+            scales = keep.tile([P, NODES], U8, name="unit_scales_%s" % label, align_bytes=64)
+            nc.vector.quantize_mx(
+                out=codes[:].bitcast(FP8X4), scales=scales[:], in_=unit_grouped[:].rearrange("p r t -> p (r t)")
+            )
+            return codes, scales
+
+        weights_low = quantise_weights(w_low_rows, LOW_PASSES, "low")
+        lo = []
+        for half in range(HALVES):
+            cam = cams.tile([P, K_PASS], F32, name="cam_low_%d" % half, tag="cam")
+            squares = stage.tile([P, HALF_SAMPLES, POSITIONS], BF16)
+            sumsq = stage.tile([P, HALF_SAMPLES], F32)
+            for pair in range(HALF_PAIRS):
+                acc = cam[:, PAIR_COLUMNS * pair : PAIR_COLUMNS * (pair + 1)]
+                for s in range(LOW_PASSES):
+                    grouped = regroup_low(raw_low[(HALF_PAIRS * half + pair, s)])
+                    add_chunk(acc, grouped, weights_low, [s] * SLABS, s == 0, s == LOW_PASSES - 1)
+                add_square_sums(sumsq, squares, cam, pair)
+            lo.append(quantise_unit_rows(cam, sumsq, WINDOW * WINDOW * EPS, "lo_%d" % half))
+
+        weights_high = quantise_weights(w_high_rows, HIGH_PASSES, "high")
+        hi = []
+        for half in range(HALVES):
+            cam = cams.tile([P, K_PASS], F32, name="cam_high_%d" % half, tag="cam")
+            squares = stage.tile([P, HALF_SAMPLES, POSITIONS], BF16)
+            sumsq = stage.tile([P, HALF_SAMPLES], F32)
+            for pair in range(HALF_PAIRS):
+                acc = cam[:, PAIR_COLUMNS * pair : PAIR_COLUMNS * (pair + 1)]
+                grouped = regroup_high(raw_high[HALF_PAIRS * half + pair])
+                add_chunk(acc, grouped, weights_high, list(range(HIGH_PASSES)), True, True)
+                add_square_sums(sumsq, squares, cam, pair)
+            hi.append(quantise_unit_rows(cam, sumsq, EPS, "hi_%d" % half))
+
+        link = links.tile([NODES, NODES], F32)
+        for half in range(HALVES):
+            nc.tensor.matmul_mx(
+                out=link[:],
+                lhsT=lo[half][0][:].bitcast(FP8X4),
+                lhsT_scale=lo[half][1][:],
+                rhs=hi[half][0][:].bitcast(FP8X4),
+                rhs_scale=hi[half][1][:],
+                start=(half == 0),
+                stop=(half == HALVES - 1),
+            )
+        result = keep.tile([NODES, NODES], F32)
+        nc.scalar.mul(result[:], link[:], 1.0 / SAMPLES)
+        nc.sync.dma_start(out=out, in_=result[:])

@@ -31,6 +31,7 @@ CHUNK = SLABS * PAIR_COLUMNS * PACK
 HALVES = SAMPLES * POSITIONS // K_PASS
 HALF_SAMPLES = SAMPLES // HALVES
 HALF_PAIRS = HALF_SAMPLES // PAIR
+RUN = 4
 
 FLOPS = 2 * NODES * SAMPLES * (C_LOW * POSITIONS * WINDOW * WINDOW + C_HIGH * POSITIONS + NODES * POSITIONS)
 
@@ -110,19 +111,20 @@ def tile_avsl_graph_pa_t_kernel(tc, fmap_low, w_low, fmap_high, w_high, out):
         def regroup_low(raw):
             grouped = stage.tile([P, CHUNK], BF16, align_bytes=64)
             source = raw[:].rearrange(
-                "p (b j yy py xx px) -> p b px yy py xx j", b=PAIR, j=PACK, yy=SIDE, py=WINDOW, xx=SIDE, px=WINDOW
+                "p (b j yy py xx px) -> p b px yy py j xx", b=PAIR, j=PACK, yy=SIDE, py=WINDOW, xx=SIDE, px=WINDOW
             )
             target = grouped[:].rearrange(
-                "p (py px b yy xx j) -> p b px yy py xx j", py=WINDOW, px=WINDOW, b=PAIR, yy=SIDE, xx=SIDE, j=PACK
+                "p (py px b yy xx j) -> p b px yy py j xx", py=WINDOW, px=WINDOW, b=PAIR, yy=SIDE, xx=SIDE, j=PACK
             )
-            nc.vector.tensor_copy(out=target[:, 0], in_=source[:, 0])
-            nc.scalar.copy(out=target[:, 1], in_=source[:, 1])
+            for px in range(WINDOW):
+                nc.vector.tensor_copy(out=target[:, 0, px], in_=source[:, 0, px])
+                nc.scalar.copy(out=target[:, 1, px], in_=source[:, 1, px])
             return grouped
 
         def regroup_high(raw):
             grouped = stage.tile([P, CHUNK], BF16, align_bytes=64)
-            source = raw[:].rearrange("p (b s j i) -> p b s i j", b=PAIR, s=HIGH_PASSES, j=PACK)
-            target = grouped[:].rearrange("p (s b i j) -> p b s i j", s=HIGH_PASSES, b=PAIR, j=PACK)
+            source = raw[:].rearrange("p (b s j c i) -> p b s c j i", b=PAIR, s=HIGH_PASSES, j=PACK, i=RUN)
+            target = grouped[:].rearrange("p (s b c i j) -> p b s c j i", s=HIGH_PASSES, b=PAIR, i=RUN, j=PACK)
             nc.vector.tensor_copy(out=target[:, 0], in_=source[:, 0])
             nc.scalar.copy(out=target[:, 1], in_=source[:, 1])
             return grouped

@@ -8,7 +8,6 @@ F32 = mybir.dt.float32
 U32 = mybir.dt.uint32
 U8 = mybir.dt.uint8
 FP8X4 = mybir.dt.float8_e4m3fn_x4
-ACT = mybir.ActivationFunctionType
 ALU = mybir.AluOpType
 
 P = 128
@@ -40,7 +39,7 @@ def tile_avsl_graph_pa_t_kernel(tc, fmap_low, w_low, fmap_high, w_high, out):
     nc = tc.nc
     with ExitStack() as stack:
         keep = stack.enter_context(tc.tile_pool(name="keep", bufs=1))
-        raws = stack.enter_context(tc.tile_pool(name="raws", bufs=(LOW_PASSES + 1) * SAMPLES // PAIR))
+        raws = stack.enter_context(tc.tile_pool(name="raws", bufs=(LOW_PASSES + 1) * SAMPLES))
         stage = stack.enter_context(tc.tile_pool(name="stage", bufs=4))
         quant = stack.enter_context(tc.tile_pool(name="quant", bufs=8))
         cams = stack.enter_context(tc.psum_pool(name="cams", bufs=2 * HALVES))
@@ -59,29 +58,37 @@ def tile_avsl_graph_pa_t_kernel(tc, fmap_low, w_low, fmap_high, w_high, out):
 
         w_low_rows = keep.tile([NODES, C_LOW], BF16)
         nc.sync.dma_start(out=w_low_rows[:], in_=w_low)
-        raw_low = {}
-        for pair in range(SAMPLES // PAIR):
-            for s in range(LOW_PASSES):
-                raw = raws.tile([P, CHUNK], BF16, name="raw_low_%d_%d" % (pair, s), tag="raw")
-                nc.sync.dma_start(
-                    out=raw[:].rearrange("p (b e) -> p b e", b=PAIR),
-                    in_=fmap_low[PAIR * pair : PAIR * (pair + 1), K_PASS * s : K_PASS * (s + 1)].rearrange(
-                        "b (p j) y x -> p b (j y x)", j=PACK
-                    ),
-                )
-                raw_low[(pair, s)] = raw
         w_high_rows = keep.tile([NODES, C_HIGH], BF16)
         nc.sync.dma_start(out=w_high_rows[:], in_=w_high)
-        raw_high = {}
-        for pair in range(SAMPLES // PAIR):
-            raw = raws.tile([P, CHUNK], BF16, name="raw_high_%d" % pair, tag="raw")
-            nc.sync.dma_start(
-                out=raw[:].rearrange("p (b s e) -> p b s e", b=PAIR, s=HIGH_PASSES),
-                in_=fmap_high[PAIR * pair : PAIR * (pair + 1)].rearrange(
-                    "b (s p j) y x -> p b s (j y x)", s=HIGH_PASSES, j=PACK
-                ),
-            )
-            raw_high[pair] = raw
+
+        banks = {}
+        chunks = []
+        for level in ("low", "high"):
+            for half in range(HALVES):
+                banks[(level, half)] = {
+                    "cam": cams.tile([P, K_PASS], F32, name="cam_%s_%d" % (level, half), tag="cam"),
+                    "squares": keep.tile([P, K_PASS], F32, name="squares_%s_%d" % (level, half)),
+                }
+                for pair in range(HALF_PAIRS):
+                    for s in range(LOW_PASSES if level == "low" else 1):
+                        raw = []
+                        for b in range(PAIR):
+                            sample = HALF_SAMPLES * half + PAIR * pair + b
+                            landing = raws.tile([P, CHUNK // PAIR], BF16, name="raw_%s_%d_%d" % (level, sample, s), tag="raw")
+                            if level == "low":
+                                nc.sync.dma_start(
+                                    out=landing[:],
+                                    in_=fmap_low[sample, K_PASS * s : K_PASS * (s + 1)].rearrange(
+                                        "(p j) y x -> p (j y x)", j=PACK
+                                    ),
+                                )
+                            else:
+                                nc.sync.dma_start(
+                                    out=landing[:].rearrange("p (s e) -> p s e", s=HIGH_PASSES),
+                                    in_=fmap_high[sample].rearrange("(s p j) y x -> p s (j y x)", s=HIGH_PASSES, j=PACK),
+                                )
+                            raw.append(landing)
+                        chunks.append({"level": level, "bank": banks[(level, half)], "pair": pair, "s": s, "raw": raw})
 
         def quantise_weights(rows, passes, level):
             words = rows[:].bitcast(F32)
@@ -96,7 +103,7 @@ def tile_avsl_graph_pa_t_kernel(tc, fmap_low, w_low, fmap_high, w_high, out):
                         nc.tensor.transpose(
                             turned[:, s, u, :], words[:, start + u : start + pass_words : 2], ident_words[:]
                         )
-                nc.vector.tensor_copy(
+                nc.scalar.copy(
                     out=grouped_words[:, first : first + 2], in_=turned[:].rearrange("p s u r -> p s r u")
                 )
             codes = keep.tile([P, passes, NODES], U32, name="w_codes_%s" % level, align_bytes=64)
@@ -108,58 +115,63 @@ def tile_avsl_graph_pa_t_kernel(tc, fmap_low, w_low, fmap_high, w_high, out):
             )
             return codes, scales
 
-        def regroup_low(raw):
+        def regroup(chunk):
             grouped = stage.tile([P, CHUNK], BF16, align_bytes=64)
-            source = raw[:].rearrange(
-                "p (b j yy py xx px) -> p b px yy py j xx", b=PAIR, j=PACK, yy=SIDE, py=WINDOW, xx=SIDE, px=WINDOW
-            )
-            target = grouped[:].rearrange(
-                "p (py px b yy xx j) -> p b px yy py j xx", py=WINDOW, px=WINDOW, b=PAIR, yy=SIDE, xx=SIDE, j=PACK
-            )
-            for px in range(WINDOW):
-                nc.vector.tensor_copy(out=target[:, 0, px], in_=source[:, 0, px])
-                nc.scalar.copy(out=target[:, 1, px], in_=source[:, 1, px])
-            return grouped
+            for b, copy in enumerate((nc.vector.tensor_copy, nc.scalar.copy)):
+                raw = chunk["raw"][b]
+                if chunk["level"] == "low":
+                    source = raw[:].rearrange(
+                        "p (j yy py xx px) -> p px yy py j xx", j=PACK, yy=SIDE, py=WINDOW, xx=SIDE, px=WINDOW
+                    )
+                    target = grouped[:].rearrange(
+                        "p (py px b yy xx j) -> p b px yy py j xx",
+                        py=WINDOW, px=WINDOW, b=PAIR, yy=SIDE, xx=SIDE, j=PACK,
+                    )
+                    for px in range(WINDOW):
+                        copy(out=target[:, b, px], in_=source[:, px])
+                else:
+                    source = raw[:].rearrange("p (s j c i) -> p s c j i", s=HIGH_PASSES, j=PACK, i=RUN)
+                    target = grouped[:].rearrange(
+                        "p (s b c i j) -> p b s c j i", s=HIGH_PASSES, b=PAIR, i=RUN, j=PACK
+                    )
+                    copy(out=target[:, b], in_=source)
+            chunk["grouped"] = grouped
 
-        def regroup_high(raw):
-            grouped = stage.tile([P, CHUNK], BF16, align_bytes=64)
-            source = raw[:].rearrange("p (b s j c i) -> p b s c j i", b=PAIR, s=HIGH_PASSES, j=PACK, i=RUN)
-            target = grouped[:].rearrange("p (s b c i j) -> p b s c j i", s=HIGH_PASSES, b=PAIR, i=RUN, j=PACK)
-            nc.vector.tensor_copy(out=target[:, 0], in_=source[:, 0])
-            nc.scalar.copy(out=target[:, 1], in_=source[:, 1])
-            return grouped
-
-        def add_chunk(acc, grouped, weights, pass_of_slab, opens, closes):
-            w_codes, w_scales = weights
+        def add_chunk(chunk):
+            low = chunk["level"] == "low"
+            w_codes, w_scales = weights[chunk["level"]]
+            pair = chunk["pair"]
             codes = quant.tile([P, SLABS, PAIR_COLUMNS], U32, align_bytes=64)
             scales = quant.tile([P, SLABS, PAIR_COLUMNS], U8, align_bytes=64)
             nc.vector.quantize_mx(
                 out=codes[:].rearrange("p m c -> p (m c)").bitcast(FP8X4),
                 scales=scales[:].rearrange("p m c -> p (m c)"),
-                in_=grouped[:],
+                in_=chunk["grouped"][:],
             )
             for slab in range(SLABS):
-                s = pass_of_slab[slab]
+                s = chunk["s"] if low else slab
                 nc.tensor.matmul_mx(
-                    out=acc,
+                    out=chunk["bank"]["cam"][:, PAIR_COLUMNS * pair : PAIR_COLUMNS * (pair + 1)],
                     lhsT=w_codes[:, s, :].bitcast(FP8X4),
                     lhsT_scale=w_scales[:, s, :],
                     rhs=codes[:, slab, :].bitcast(FP8X4),
                     rhs_scale=scales[:, slab, :],
-                    start=(opens and slab == 0),
-                    stop=(closes and slab == SLABS - 1),
+                    start=(slab == 0 and chunk["s"] == 0),
+                    stop=(slab == SLABS - 1 and closes_pair(chunk)),
                 )
 
-        def add_square_sums(sumsq, squares, cam, pair):
-            for b in range(PAIR * pair, PAIR * (pair + 1)):
-                nc.scalar.activation(
-                    out=squares[:, b, :],
-                    in_=cam[:, POSITIONS * b : POSITIONS * (b + 1)],
-                    func=ACT.Square,
-                    accum_out=sumsq[:, b : b + 1],
-                )
+        def closes_pair(chunk):
+            return chunk["level"] == "high" or chunk["s"] == LOW_PASSES - 1
 
-        def quantise_unit_rows(cam, sumsq, floor, label):
+        def square_pair(bank, pair):
+            columns = slice(PAIR_COLUMNS * pair, PAIR_COLUMNS * (pair + 1))
+            nc.scalar.square(bank["squares"][:, columns], bank["cam"][:, columns])
+
+        def quantise_unit_rows(cam, squares, floor, label):
+            sumsq = stage.tile([P, HALF_SAMPLES], F32)
+            nc.vector.reduce_sum(
+                out=sumsq[:], in_=squares[:].rearrange("p (b i) -> p b i", i=POSITIONS), axis=mybir.AxisListType.X
+            )
             floored = stage.tile([P, HALF_SAMPLES], F32)
             nc.vector.tensor_scalar_max(out=floored[:], in0=sumsq[:], scalar1=floor * floor)
             norm = stage.tile([P, HALF_SAMPLES], F32)
@@ -185,32 +197,29 @@ def tile_avsl_graph_pa_t_kernel(tc, fmap_low, w_low, fmap_high, w_high, out):
             )
             return codes, scales
 
-        weights_low = quantise_weights(w_low_rows, LOW_PASSES, "low")
-        lo = []
-        for half in range(HALVES):
-            cam = cams.tile([P, K_PASS], F32, name="cam_low_%d" % half, tag="cam")
-            squares = stage.tile([P, HALF_SAMPLES, POSITIONS], BF16)
-            sumsq = stage.tile([P, HALF_SAMPLES], F32)
-            for pair in range(HALF_PAIRS):
-                acc = cam[:, PAIR_COLUMNS * pair : PAIR_COLUMNS * (pair + 1)]
-                for s in range(LOW_PASSES):
-                    grouped = regroup_low(raw_low[(HALF_PAIRS * half + pair, s)])
-                    add_chunk(acc, grouped, weights_low, [s] * SLABS, s == 0, s == LOW_PASSES - 1)
-                add_square_sums(sumsq, squares, cam, pair)
-            lo.append(quantise_unit_rows(cam, sumsq, WINDOW * WINDOW * EPS, "lo_%d" % half))
+        weights = {
+            "low": quantise_weights(w_low_rows, LOW_PASSES, "low"),
+            "high": quantise_weights(w_high_rows, HIGH_PASSES, "high"),
+        }
 
-        weights_high = quantise_weights(w_high_rows, HIGH_PASSES, "high")
-        hi = []
-        for half in range(HALVES):
-            cam = cams.tile([P, K_PASS], F32, name="cam_high_%d" % half, tag="cam")
-            squares = stage.tile([P, HALF_SAMPLES, POSITIONS], BF16)
-            sumsq = stage.tile([P, HALF_SAMPLES], F32)
-            for pair in range(HALF_PAIRS):
-                acc = cam[:, PAIR_COLUMNS * pair : PAIR_COLUMNS * (pair + 1)]
-                grouped = regroup_high(raw_high[HALF_PAIRS * half + pair])
-                add_chunk(acc, grouped, weights_high, list(range(HIGH_PASSES)), True, True)
-                add_square_sums(sumsq, squares, cam, pair)
-            hi.append(quantise_unit_rows(cam, sumsq, EPS, "hi_%d" % half))
+        for step in range(len(chunks) + 2):
+            if step < len(chunks):
+                regroup(chunks[step])
+            if 1 <= step <= len(chunks):
+                add_chunk(chunks[step - 1])
+            if step >= 2 and closes_pair(chunks[step - 2]):
+                square_pair(chunks[step - 2]["bank"], chunks[step - 2]["pair"])
+
+        floors = {"low": WINDOW * WINDOW * EPS, "high": EPS}
+        units = {}
+        for level in ("low", "high"):
+            for half in range(HALVES):
+                bank = banks[(level, half)]
+                units[(level, half)] = quantise_unit_rows(
+                    bank["cam"], bank["squares"], floors[level], "%s_%d" % (level, half)
+                )
+        lo = [units[("low", half)] for half in range(HALVES)]
+        hi = [units[("high", half)] for half in range(HALVES)]
 
         link = links.tile([NODES, NODES], F32)
         for half in range(HALVES):

@@ -8,6 +8,7 @@ F32 = mybir.dt.float32
 U32 = mybir.dt.uint32
 U8 = mybir.dt.uint8
 FP8X4 = mybir.dt.float8_e4m3fn_x4
+ACT = mybir.ActivationFunctionType
 ALU = mybir.AluOpType
 
 P = 128
@@ -66,8 +67,10 @@ def tile_avsl_graph_pa_t_kernel(tc, fmap_low, w_low, fmap_high, w_high, out):
         for level in ("low", "high"):
             for half in range(HALVES):
                 banks[(level, half)] = {
+                    "label": "%s_%d" % (level, half),
                     "cam": cams.tile([P, K_PASS], F32, name="cam_%s_%d" % (level, half), tag="cam"),
-                    "squares": keep.tile([P, K_PASS], F32, name="squares_%s_%d" % (level, half)),
+                    "squares": keep.tile([P, HALF_SAMPLES, POSITIONS], BF16, name="squares_%s_%d" % (level, half)),
+                    "sumsq": keep.tile([P, HALF_SAMPLES], F32, name="sumsq_%s_%d" % (level, half)),
                 }
                 for pair in range(HALF_PAIRS):
                     for s in range(LOW_PASSES if level == "low" else 1):
@@ -103,7 +106,7 @@ def tile_avsl_graph_pa_t_kernel(tc, fmap_low, w_low, fmap_high, w_high, out):
                         nc.tensor.transpose(
                             turned[:, s, u, :], words[:, start + u : start + pass_words : 2], ident_words[:]
                         )
-                nc.scalar.copy(
+                nc.vector.tensor_copy(
                     out=grouped_words[:, first : first + 2], in_=turned[:].rearrange("p s u r -> p s r u")
                 )
             codes = keep.tile([P, passes, NODES], U32, name="w_codes_%s" % level, align_bytes=64)
@@ -163,15 +166,16 @@ def tile_avsl_graph_pa_t_kernel(tc, fmap_low, w_low, fmap_high, w_high, out):
         def closes_pair(chunk):
             return chunk["level"] == "high" or chunk["s"] == LOW_PASSES - 1
 
-        def square_pair(bank, pair):
-            columns = slice(PAIR_COLUMNS * pair, PAIR_COLUMNS * (pair + 1))
-            nc.scalar.square(bank["squares"][:, columns], bank["cam"][:, columns])
+        def add_square_sums(sumsq, squares, cam, pair):
+            for b in range(PAIR * pair, PAIR * (pair + 1)):
+                nc.scalar.activation(
+                    out=squares[:, b, :],
+                    in_=cam[:, POSITIONS * b : POSITIONS * (b + 1)],
+                    func=ACT.Square,
+                    accum_out=sumsq[:, b : b + 1],
+                )
 
-        def quantise_unit_rows(cam, squares, floor, label):
-            sumsq = stage.tile([P, HALF_SAMPLES], F32)
-            nc.vector.reduce_sum(
-                out=sumsq[:], in_=squares[:].rearrange("p (b i) -> p b i", i=POSITIONS), axis=mybir.AxisListType.X
-            )
+        def quantise_unit_rows(cam, sumsq, floor, label):
             floored = stage.tile([P, HALF_SAMPLES], F32)
             nc.vector.tensor_scalar_max(out=floored[:], in0=sumsq[:], scalar1=floor * floor)
             norm = stage.tile([P, HALF_SAMPLES], F32)
@@ -202,24 +206,23 @@ def tile_avsl_graph_pa_t_kernel(tc, fmap_low, w_low, fmap_high, w_high, out):
             "high": quantise_weights(w_high_rows, HIGH_PASSES, "high"),
         }
 
+        floors = {"low": WINDOW * WINDOW * EPS, "high": EPS}
+        units = {}
         for step in range(len(chunks) + 2):
             if step < len(chunks):
                 regroup(chunks[step])
             if 1 <= step <= len(chunks):
                 add_chunk(chunks[step - 1])
             if step >= 2 and closes_pair(chunks[step - 2]):
-                square_pair(chunks[step - 2]["bank"], chunks[step - 2]["pair"])
-
-        floors = {"low": WINDOW * WINDOW * EPS, "high": EPS}
-        units = {}
-        for level in ("low", "high"):
-            for half in range(HALVES):
-                bank = banks[(level, half)]
-                units[(level, half)] = quantise_unit_rows(
-                    bank["cam"], bank["squares"], floors[level], "%s_%d" % (level, half)
-                )
-        lo = [units[("low", half)] for half in range(HALVES)]
-        hi = [units[("high", half)] for half in range(HALVES)]
+                done = chunks[step - 2]
+                bank = done["bank"]
+                add_square_sums(bank["sumsq"], bank["squares"], bank["cam"], done["pair"])
+                if done["pair"] == HALF_PAIRS - 1:
+                    units[bank["label"]] = quantise_unit_rows(
+                        bank["cam"], bank["sumsq"], floors[done["level"]], bank["label"]
+                    )
+        lo = [units["low_%d" % half] for half in range(HALVES)]
+        hi = [units["high_%d" % half] for half in range(HALVES)]
 
         link = links.tile([NODES, NODES], F32)
         for half in range(HALVES):

@@ -31,6 +31,7 @@ CHUNK = SLABS * PAIR_COLUMNS * PACK
 HALVES = SAMPLES * POSITIONS // K_PASS
 HALF_SAMPLES = SAMPLES // HALVES
 HALF_PAIRS = HALF_SAMPLES // PAIR
+VECTOR_EXTRA = ()
 RUN = 4
 
 FLOPS = 2 * NODES * SAMPLES * (C_LOW * POSITIONS * WINDOW * WINDOW + C_HIGH * POSITIONS + NODES * POSITIONS)
@@ -41,12 +42,13 @@ def tile_avsl_graph_pa_t_kernel(tc, fmap_low, w_low, fmap_high, w_high, out):
     with ExitStack() as stack:
         keep = stack.enter_context(tc.tile_pool(name="keep", bufs=1))
         raws = stack.enter_context(tc.tile_pool(name="raws", bufs=(LOW_PASSES + 1) * SAMPLES))
-        stage = stack.enter_context(tc.tile_pool(name="stage", bufs=4))
+        stage = stack.enter_context(tc.tile_pool(name="stage", bufs=6))
         quant = stack.enter_context(tc.tile_pool(name="quant", bufs=8))
         cams = stack.enter_context(tc.psum_pool(name="cams", bufs=2 * HALVES))
         turns = stack.enter_context(tc.psum_pool(name="turns", bufs=3))
         links = stack.enter_context(tc.psum_pool(name="links", bufs=1))
 
+        stack.enter_context(tc.manual_schedule())
         ident_words = keep.tile([P, P], F32)
         make_identity(nc, ident_words[:])
         ident_bf16 = keep.tile([P, P], BF16)
@@ -55,45 +57,52 @@ def tile_avsl_graph_pa_t_kernel(tc, fmap_low, w_low, fmap_high, w_high, out):
         one = keep.tile([P, 1], F32)
         nc.vector.memset(one[:], 1.0)
         root_of_one = keep.tile([P, 1], F32)
-        nc.scalar.sqrt(root_of_one[:], one[:])
+        nc.scalar.activation(out=root_of_one[:], in_=one[:], func=ACT.Abs_reciprocal_sqrt)
 
         w_low_rows = keep.tile([NODES, C_LOW], BF16)
-        nc.sync.dma_start(out=w_low_rows[:], in_=w_low)
         w_high_rows = keep.tile([NODES, C_HIGH], BF16)
-        nc.sync.dma_start(out=w_high_rows[:], in_=w_high)
-
         banks = {}
         chunks = []
         for level in ("low", "high"):
             for half in range(HALVES):
                 banks[(level, half)] = {
                     "label": "%s_%d" % (level, half),
+                    "level": level,
                     "cam": cams.tile([P, K_PASS], F32, name="cam_%s_%d" % (level, half), tag="cam"),
                     "squares": keep.tile([P, HALF_SAMPLES, POSITIONS], BF16, name="squares_%s_%d" % (level, half)),
                     "sumsq": keep.tile([P, HALF_SAMPLES], F32, name="sumsq_%s_%d" % (level, half)),
+                    "inverse": keep.tile([P, HALF_SAMPLES], F32, name="inverse_%s_%d" % (level, half)),
+                    "unit": keep.tile([P, K_PASS], BF16, name="unit_%s_%d" % (level, half)),
+                    "unit_grouped": keep.tile([P, NODES, PACK], BF16, name="unit_grouped_%s_%d" % (level, half), align_bytes=64),
                 }
                 for pair in range(HALF_PAIRS):
                     for s in range(LOW_PASSES if level == "low" else 1):
-                        raw = []
-                        for b in range(PAIR):
-                            sample = HALF_SAMPLES * half + PAIR * pair + b
-                            landing = raws.tile([P, CHUNK // PAIR], BF16, name="raw_%s_%d_%d" % (level, sample, s), tag="raw")
-                            if level == "low":
-                                nc.sync.dma_start(
-                                    out=landing[:],
-                                    in_=fmap_low[sample, K_PASS * s : K_PASS * (s + 1)].rearrange(
-                                        "(p j) y x -> p (j y x)", j=PACK
-                                    ),
-                                )
-                            else:
-                                nc.sync.dma_start(
-                                    out=landing[:].rearrange("p (s e) -> p s e", s=HIGH_PASSES),
-                                    in_=fmap_high[sample].rearrange("(s p j) y x -> p s (j y x)", s=HIGH_PASSES, j=PACK),
-                                )
-                            raw.append(landing)
-                        chunks.append({"level": level, "bank": banks[(level, half)], "pair": pair, "s": s, "raw": raw})
+                        chunks.append({"level": level, "bank": banks[(level, half)], "pair": pair, "s": s, "n": len(chunks), "sample": HALF_SAMPLES * half + PAIR * pair})
+        for n, chunk in enumerate(chunks):
+            if n == 1:
+                nc.sync.dma_start(out=w_low_rows[:], in_=w_low)
+            if n == 8:
+                nc.sync.dma_start(out=w_high_rows[:], in_=w_high)
+            chunk["raw"] = []
+            for b in range(PAIR):
+                sample = chunk["sample"] + b
+                s = chunk["s"]
+                landing = raws.tile([P, CHUNK // PAIR], BF16, name="raw_%d_%d" % (n, b), tag="raw")
+                if chunk["level"] == "low":
+                    nc.sync.dma_start(
+                        out=landing[:],
+                        in_=fmap_low[sample, K_PASS * s : K_PASS * (s + 1)].rearrange(
+                            "(p j) y x -> p (j y x)", j=PACK
+                        ),
+                    )
+                else:
+                    nc.sync.dma_start(
+                        out=landing[:].rearrange("p (s e) -> p s e", s=HIGH_PASSES),
+                        in_=fmap_high[sample].rearrange("(s p j) y x -> p s (j y x)", s=HIGH_PASSES, j=PACK),
+                    )
+                chunk["raw"].append(landing)
 
-        def quantise_weights(rows, passes, level):
+        def turn_weights(rows, passes, level):
             words = rows[:].bitcast(F32)
             pass_words = K_PASS // 2
             grouped = keep.tile([P, passes * NODES * PACK], BF16, name="w_grouped_%s" % level, align_bytes=64)
@@ -109,6 +118,9 @@ def tile_avsl_graph_pa_t_kernel(tc, fmap_low, w_low, fmap_high, w_high, out):
                 nc.vector.tensor_copy(
                     out=grouped_words[:, first : first + 2], in_=turned[:].rearrange("p s u r -> p s r u")
                 )
+            return grouped
+
+        def quantise_turned_weights(grouped, passes, level):
             codes = keep.tile([P, passes, NODES], U32, name="w_codes_%s" % level, align_bytes=64)
             scales = keep.tile([P, passes, NODES], U8, name="w_scales_%s" % level, align_bytes=64)
             nc.vector.quantize_mx(
@@ -116,10 +128,10 @@ def tile_avsl_graph_pa_t_kernel(tc, fmap_low, w_low, fmap_high, w_high, out):
                 scales=scales[:].rearrange("p s r -> p (s r)"),
                 in_=grouped[:],
             )
-            return codes, scales
+            weights[level] = (codes, scales)
 
         def regroup(chunk):
-            grouped = stage.tile([P, CHUNK], BF16, align_bytes=64)
+            grouped = stage.tile([P, CHUNK], BF16, name="grouped", tag="grouped", align_bytes=64)
             for b, copy in enumerate((nc.vector.tensor_copy, nc.scalar.copy)):
                 raw = chunk["raw"][b]
                 if chunk["level"] == "low":
@@ -131,7 +143,10 @@ def tile_avsl_graph_pa_t_kernel(tc, fmap_low, w_low, fmap_high, w_high, out):
                         py=WINDOW, px=WINDOW, b=PAIR, yy=SIDE, xx=SIDE, j=PACK,
                     )
                     for px in range(WINDOW):
-                        copy(out=target[:, b, px], in_=source[:, px])
+                        if chunk["n"] in VECTOR_EXTRA and b == 1 and px == 0:
+                            nc.vector.tensor_copy(out=target[:, b, px], in_=source[:, px])
+                        else:
+                            copy(out=target[:, b, px], in_=source[:, px])
                 else:
                     source = raw[:].rearrange("p (s j c i) -> p s c j i", s=HIGH_PASSES, j=PACK, i=RUN)
                     target = grouped[:].rearrange(
@@ -140,17 +155,21 @@ def tile_avsl_graph_pa_t_kernel(tc, fmap_low, w_low, fmap_high, w_high, out):
                     copy(out=target[:, b], in_=source)
             chunk["grouped"] = grouped
 
-        def add_chunk(chunk):
-            low = chunk["level"] == "low"
-            w_codes, w_scales = weights[chunk["level"]]
-            pair = chunk["pair"]
-            codes = quant.tile([P, SLABS, PAIR_COLUMNS], U32, align_bytes=64)
-            scales = quant.tile([P, SLABS, PAIR_COLUMNS], U8, align_bytes=64)
+        def quantise_chunk(chunk):
+            codes = quant.tile([P, SLABS, PAIR_COLUMNS], U32, name="codes", tag="codes", align_bytes=64)
+            scales = quant.tile([P, SLABS, PAIR_COLUMNS], U8, name="scales", tag="scales", align_bytes=64)
             nc.vector.quantize_mx(
                 out=codes[:].rearrange("p m c -> p (m c)").bitcast(FP8X4),
                 scales=scales[:].rearrange("p m c -> p (m c)"),
                 in_=chunk["grouped"][:],
             )
+            chunk["codes"], chunk["scales"] = codes, scales
+
+        def multiply_chunk(chunk):
+            low = chunk["level"] == "low"
+            w_codes, w_scales = weights[chunk["level"]]
+            pair = chunk["pair"]
+            codes, scales = chunk["codes"], chunk["scales"]
             for slab in range(SLABS):
                 s = chunk["s"] if low else slab
                 nc.tensor.matmul_mx(
@@ -166,61 +185,95 @@ def tile_avsl_graph_pa_t_kernel(tc, fmap_low, w_low, fmap_high, w_high, out):
         def closes_pair(chunk):
             return chunk["level"] == "high" or chunk["s"] == LOW_PASSES - 1
 
-        def add_square_sums(sumsq, squares, cam, pair):
-            for b in range(PAIR * pair, PAIR * (pair + 1)):
+        def add_square_sums(bank, pairs):
+            for b in range(PAIR * pairs.start, PAIR * pairs.stop):
                 nc.scalar.activation(
-                    out=squares[:, b, :],
-                    in_=cam[:, POSITIONS * b : POSITIONS * (b + 1)],
+                    out=bank["squares"][:, b, :],
+                    in_=bank["cam"][:, POSITIONS * b : POSITIONS * (b + 1)],
                     func=ACT.Square,
-                    accum_out=sumsq[:, b : b + 1],
+                    accum_out=bank["sumsq"][:, b : b + 1],
                 )
 
-        def quantise_unit_rows(cam, sumsq, floor, label):
-            floored = stage.tile([P, HALF_SAMPLES], F32)
-            nc.vector.tensor_scalar_max(out=floored[:], in0=sumsq[:], scalar1=floor * floor)
-            norm = stage.tile([P, HALF_SAMPLES], F32)
-            nc.scalar.sqrt(norm[:], floored[:])
-            inverse = stage.tile([P, HALF_SAMPLES], F32)
-            nc.vector.reciprocal(inverse[:], norm[:])
-            unit = stage.tile([P, K_PASS], BF16)
-            nc.vector.tensor_tensor(
-                out=unit[:].rearrange("p (b i) -> p b i", i=POSITIONS),
-                in0=cam[:].rearrange("p (b i) -> p b i", i=POSITIONS),
-                in1=inverse[:].unsqueeze(2).to_broadcast([P, HALF_SAMPLES, POSITIONS]),
-                op=ALU.mult,
+        def root_norms(bank, pairs):
+            span = slice(PAIR * pairs.start, PAIR * pairs.stop)
+            nc.scalar.activation(out=bank["inverse"][:, span], in_=bank["sumsq"][:, span], func=ACT.Abs_reciprocal_sqrt)
+
+        def divide_by_norms(bank, pairs):
+            span = slice(PAIR * pairs.start, PAIR * pairs.stop)
+            columns = slice(PAIR_COLUMNS * pairs.start, PAIR_COLUMNS * pairs.stop)
+            samples = PAIR * len(pairs)
+            floor = WINDOW * WINDOW * EPS if bank["level"] == "low" else EPS
+            inverse = bank["inverse"]
+            nc.vector.scalar_tensor_tensor(
+                out=bank["unit"][:, columns].rearrange("p (b i) -> p b i", i=POSITIONS),
+                in0=inverse[:, span].unsqueeze(2).to_broadcast([P, samples, POSITIONS]),
+                scalar=1.0 / floor,
+                in1=bank["cam"][:, columns].rearrange("p (b i) -> p b i", i=POSITIONS),
+                op0=ALU.min,
+                op1=ALU.mult,
             )
-            turned = turns.tile([P, PACK, NODES], BF16, tag="turn")
-            for t in range(PACK):
-                nc.tensor.transpose(turned[:, t, :], unit[:, P * t : P * (t + 1)], ident_bf16[:])
-            unit_grouped = stage.tile([P, NODES, PACK], BF16, align_bytes=64)
-            nc.scalar.copy(out=unit_grouped[:], in_=turned[:].rearrange("p t r -> p r t"))
-            codes = keep.tile([P, NODES], U32, name="unit_codes_%s" % label, align_bytes=64)
-            scales = keep.tile([P, NODES], U8, name="unit_scales_%s" % label, align_bytes=64)
+
+        def turn_units(bank, pairs):
+            if pairs.start == 0:
+                turned = turns.tile([P, PACK, NODES], BF16, name="unit_turned", tag="turn")
+                bank["turned"] = turned
+            for t in pairs:
+                nc.tensor.transpose(bank["turned"][:, t, :], bank["unit"][:, P * t : P * (t + 1)], ident_bf16[:])
+
+        def regroup_units(bank, pairs):
+            nc.scalar.copy(out=bank["unit_grouped"][:], in_=bank["turned"][:].rearrange("p t r -> p r t"))
+
+        def quantise_units(bank, pairs):
+            codes = keep.tile([P, NODES], U32, name="unit_codes_%s" % bank["label"], align_bytes=64)
+            scales = keep.tile([P, NODES], U8, name="unit_scales_%s" % bank["label"], align_bytes=64)
             nc.vector.quantize_mx(
-                out=codes[:].bitcast(FP8X4), scales=scales[:], in_=unit_grouped[:].rearrange("p r t -> p (r t)")
+                out=codes[:].bitcast(FP8X4), scales=scales[:],
+                in_=bank["unit_grouped"][:].rearrange("p r t -> p (r t)"),
             )
-            return codes, scales
+            units[bank["label"]] = (codes, scales)
 
-        weights = {
-            "low": quantise_weights(w_low_rows, LOW_PASSES, "low"),
-            "high": quantise_weights(w_high_rows, HIGH_PASSES, "high"),
-        }
-
-        floors = {"low": WINDOW * WINDOW * EPS, "high": EPS}
+        weights = {}
         units = {}
-        for step in range(len(chunks) + 2):
+        turned_weights = {}
+        later = {}
+
+        def plan(step, task, bank, pairs):
+            later.setdefault(step, []).append((task, bank, pairs))
+
+        QLAG, MLAG, SLAG = 1, 2, 2
+        for step in range(len(chunks) + 12):
+            if MLAG <= step < len(chunks) + MLAG:
+                done = chunks[step - MLAG]
+                multiply_chunk(done)
+                if closes_pair(done):
+                    bank, pair = done["bank"], done["pair"]
+                    tail = bank is chunks[-1]["bank"]
+                    whole = pair == HALF_PAIRS - 1
+                    at = step + SLAG
+                    plan(at, add_square_sums, bank, range(pair, pair + 1))
+                    if tail or whole:
+                        pairs = range(pair, pair + 1) if tail else range(HALF_PAIRS)
+                        plan(at, root_norms, bank, pairs)
+                        plan(at + 1, divide_by_norms, bank, pairs)
+                        plan(at + 2, turn_units, bank, pairs)
+                    if whole:
+                        plan(at + 3, regroup_units, bank, None)
+                        plan(at + 4, quantise_units, bank, None)
             if step < len(chunks):
                 regroup(chunks[step])
-            if 1 <= step <= len(chunks):
-                add_chunk(chunks[step - 1])
-            if step >= 2 and closes_pair(chunks[step - 2]):
-                done = chunks[step - 2]
-                bank = done["bank"]
-                add_square_sums(bank["sumsq"], bank["squares"], bank["cam"], done["pair"])
-                if done["pair"] == HALF_PAIRS - 1:
-                    units[bank["label"]] = quantise_unit_rows(
-                        bank["cam"], bank["sumsq"], floors[done["level"]], bank["label"]
-                    )
+            if step == 0:
+                turned_weights["low"] = turn_weights(w_low_rows, LOW_PASSES, "low")
+            if step == 1:
+                quantise_turned_weights(turned_weights["low"], LOW_PASSES, "low")
+            if step == 10:
+                turned_weights["high"] = turn_weights(w_high_rows, HIGH_PASSES, "high")
+            if step == 11:
+                quantise_turned_weights(turned_weights["high"], HIGH_PASSES, "high")
+            if QLAG <= step < len(chunks) + QLAG:
+                quantise_chunk(chunks[step - QLAG])
+            for task, bank, pairs in later.pop(step, []):
+                task(bank, pairs)
+
         lo = [units["low_%d" % half] for half in range(HALVES)]
         hi = [units["high_%d" % half] for half in range(HALVES)]
 

@@ -41,7 +41,7 @@ def tile_avsl_graph_pa_t_kernel(tc, fmap_low, w_low, fmap_high, w_high, out):
     nc = tc.nc
     with ExitStack() as stack:
         keep = stack.enter_context(tc.tile_pool(name="keep", bufs=1))
-        raws = stack.enter_context(tc.tile_pool(name="raws", bufs=(LOW_PASSES + 1) * SAMPLES))
+        raws = stack.enter_context(tc.tile_pool(name="raws", bufs=(LOW_PASSES + 1) * SAMPLES // PAIR))
         stage = stack.enter_context(tc.tile_pool(name="stage", bufs=6))
         quant = stack.enter_context(tc.tile_pool(name="quant", bufs=8))
         cams = stack.enter_context(tc.psum_pool(name="cams", bufs=2 * HALVES))
@@ -83,24 +83,26 @@ def tile_avsl_graph_pa_t_kernel(tc, fmap_low, w_low, fmap_high, w_high, out):
                 nc.sync.dma_start(out=w_low_rows[:], in_=w_low)
             if n == 8:
                 nc.sync.dma_start(out=w_high_rows[:], in_=w_high)
-            chunk["raw"] = []
-            for b in range(PAIR):
-                sample = chunk["sample"] + b
-                s = chunk["s"]
-                landing = raws.tile([P, CHUNK // PAIR], BF16, name="raw_%d_%d" % (n, b), tag="raw")
+            landing = raws.tile([P, PAIR, CHUNK // PAIR], BF16, name="raw_%d" % n, tag="raw")
+            samples = slice(chunk["sample"], chunk["sample"] + PAIR)
+            s = chunk["s"]
+            pieces = [slice(b, b + 1) for b in range(PAIR)] if n in (0,) else [slice(0, PAIR)]
+            for piece in pieces:
+                source = slice(chunk["sample"] + piece.start, chunk["sample"] + piece.stop)
                 if chunk["level"] == "low":
                     nc.sync.dma_start(
-                        out=landing[:],
-                        in_=fmap_low[sample, K_PASS * s : K_PASS * (s + 1)].rearrange(
-                            "(p j) y x -> p (j y x)", j=PACK
+                        out=landing[:, piece],
+                        in_=fmap_low[source, K_PASS * s : K_PASS * (s + 1)].rearrange(
+                            "b (p j) y x -> p b (j y x)", j=PACK
                         ),
                     )
                 else:
-                    nc.sync.dma_start(
-                        out=landing[:].rearrange("p (s e) -> p s e", s=HIGH_PASSES),
-                        in_=fmap_high[sample].rearrange("(s p j) y x -> p s (j y x)", s=HIGH_PASSES, j=PACK),
-                    )
-                chunk["raw"].append(landing)
+                    for b in range(piece.start, piece.stop):
+                        nc.sync.dma_start(
+                            out=landing[:, b].rearrange("p (s e) -> p s e", s=HIGH_PASSES),
+                            in_=fmap_high[chunk["sample"] + b].rearrange("(s p j) y x -> p s (j y x)", s=HIGH_PASSES, j=PACK),
+                        )
+            chunk["raw"] = [landing[:, b, :] for b in range(PAIR)]
 
         def turn_weights(rows, passes, level):
             words = rows[:].bitcast(F32)
@@ -135,7 +137,7 @@ def tile_avsl_graph_pa_t_kernel(tc, fmap_low, w_low, fmap_high, w_high, out):
             for b, copy in enumerate((nc.vector.tensor_copy, nc.scalar.copy)):
                 raw = chunk["raw"][b]
                 if chunk["level"] == "low":
-                    source = raw[:].rearrange(
+                    source = raw.rearrange(
                         "p (j yy py xx px) -> p px yy py j xx", j=PACK, yy=SIDE, py=WINDOW, xx=SIDE, px=WINDOW
                     )
                     target = grouped[:].rearrange(
@@ -148,7 +150,7 @@ def tile_avsl_graph_pa_t_kernel(tc, fmap_low, w_low, fmap_high, w_high, out):
                         else:
                             copy(out=target[:, b, px], in_=source[:, px])
                 else:
-                    source = raw[:].rearrange("p (s j c i) -> p s c j i", s=HIGH_PASSES, j=PACK, i=RUN)
+                    source = raw.rearrange("p (s j c i) -> p s c j i", s=HIGH_PASSES, j=PACK, i=RUN)
                     target = grouped[:].rearrange(
                         "p (s b c i j) -> p b s c j i", s=HIGH_PASSES, b=PAIR, i=RUN, j=PACK
                     )

@@ -45,14 +45,16 @@ def tile_avsl_graph_pa_t_kernel(tc, fmap_low, w_low, fmap_high, w_high, out):
         stage = stack.enter_context(tc.tile_pool(name="stage", bufs=6))
         quant = stack.enter_context(tc.tile_pool(name="quant", bufs=8))
         cams = stack.enter_context(tc.psum_pool(name="cams", bufs=2 * HALVES))
-        turns = stack.enter_context(tc.psum_pool(name="turns", bufs=3))
-        links = stack.enter_context(tc.psum_pool(name="links", bufs=1))
+        turns = stack.enter_context(tc.psum_pool(name="turns", bufs=4))
 
         stack.enter_context(tc.manual_schedule())
         ident_words = keep.tile([P, P], F32)
         make_identity(nc, ident_words[:])
-        ident_bf16 = keep.tile([P, P], BF16)
-        make_identity(nc, ident_bf16[:])
+        same_sample = keep.tile([P, P], F32)
+        nc.gpsimd.memset(same_sample[:], 0.0)
+        for b in range(PAIR):
+            rows = slice(POSITIONS * b, POSITIONS * (b + 1))
+            nc.gpsimd.memset(same_sample[rows, rows], 1.0)
 
         one = keep.tile([P, 1], F32)
         nc.vector.memset(one[:], 1.0)
@@ -69,11 +71,9 @@ def tile_avsl_graph_pa_t_kernel(tc, fmap_low, w_low, fmap_high, w_high, out):
                     "label": "%s_%d" % (level, half),
                     "level": level,
                     "cam": cams.tile([P, K_PASS], F32, name="cam_%s_%d" % (level, half), tag="cam"),
-                    "squares": keep.tile([P, HALF_SAMPLES, POSITIONS], BF16, name="squares_%s_%d" % (level, half)),
-                    "sumsq": keep.tile([P, HALF_SAMPLES], F32, name="sumsq_%s_%d" % (level, half)),
-                    "inverse": keep.tile([P, HALF_SAMPLES], F32, name="inverse_%s_%d" % (level, half)),
-                    "unit": keep.tile([P, K_PASS], BF16, name="unit_%s_%d" % (level, half)),
-                    "unit_grouped": keep.tile([P, NODES, PACK], BF16, name="unit_grouped_%s_%d" % (level, half), align_bytes=64),
+                    "squares": keep.tile([P, K_PASS], F32, name="squares_%s_%d" % (level, half)),
+                    "inverse": keep.tile([P, NODES, PACK], F32, name="inverse_%s_%d" % (level, half)),
+                    "unit": keep.tile([P, NODES, PACK], BF16, name="unit_%s_%d" % (level, half), align_bytes=64),
                 }
                 for pair in range(HALF_PAIRS):
                     for s in range(LOW_PASSES if level == "low" else 1):
@@ -176,10 +176,10 @@ def tile_avsl_graph_pa_t_kernel(tc, fmap_low, w_low, fmap_high, w_high, out):
                 s = chunk["s"] if low else slab
                 nc.tensor.matmul_mx(
                     out=chunk["bank"]["cam"][:, PAIR_COLUMNS * pair : PAIR_COLUMNS * (pair + 1)],
-                    lhsT=w_codes[:, s, :].bitcast(FP8X4),
-                    lhsT_scale=w_scales[:, s, :],
-                    rhs=codes[:, slab, :].bitcast(FP8X4),
-                    rhs_scale=scales[:, slab, :],
+                    lhsT=codes[:, slab, :].bitcast(FP8X4),
+                    lhsT_scale=scales[:, slab, :],
+                    rhs=w_codes[:, s, :].bitcast(FP8X4),
+                    rhs_scale=w_scales[:, s, :],
                     start=(slab == 0 and chunk["s"] == 0),
                     stop=(slab == SLABS - 1 and closes_pair(chunk)),
                 )
@@ -187,50 +187,43 @@ def tile_avsl_graph_pa_t_kernel(tc, fmap_low, w_low, fmap_high, w_high, out):
         def closes_pair(chunk):
             return chunk["level"] == "high" or chunk["s"] == LOW_PASSES - 1
 
-        def add_square_sums(bank, pairs):
-            for b in range(PAIR * pairs.start, PAIR * pairs.stop):
-                nc.scalar.activation(
-                    out=bank["squares"][:, b, :],
-                    in_=bank["cam"][:, POSITIONS * b : POSITIONS * (b + 1)],
-                    func=ACT.Square,
-                    accum_out=bank["sumsq"][:, b : b + 1],
-                )
+        def square_maps(bank, pairs):
+            columns = slice(NODES * pairs.start, NODES * pairs.stop)
+            nc.scalar.activation(out=bank["squares"][:, columns], in_=bank["cam"][:, columns], func=ACT.Square)
 
-        def root_norms(bank, pairs):
-            span = slice(PAIR * pairs.start, PAIR * pairs.stop)
-            nc.scalar.activation(out=bank["inverse"][:, span], in_=bank["sumsq"][:, span], func=ACT.Abs_reciprocal_sqrt)
+        def sum_squares(bank, pairs):
+            columns = slice(NODES * pairs.start, NODES * pairs.stop)
+            if pairs.start == 0:
+                sums = turns.tile([P, K_PASS], F32, name="sums", tag="turn")
+                bank["sums"] = sums
+            nc.tensor.matmul(
+                bank["sums"][:, columns], lhsT=same_sample[:], rhs=bank["squares"][:, columns], start=True, stop=True
+            )
 
-        def divide_by_norms(bank, pairs):
-            span = slice(PAIR * pairs.start, PAIR * pairs.stop)
-            columns = slice(PAIR_COLUMNS * pairs.start, PAIR_COLUMNS * pairs.stop)
-            samples = PAIR * len(pairs)
+        def invert_norms(bank, nodes):
+            nc.scalar.activation(
+                out=bank["inverse"][:, nodes, :],
+                in_=bank["sums"][:].rearrange("p (t r) -> p r t", t=PACK)[:, nodes, :],
+                func=ACT.Abs_reciprocal_sqrt,
+            )
+
+        def divide_by_norms(bank, nodes):
             floor = WINDOW * WINDOW * EPS if bank["level"] == "low" else EPS
-            inverse = bank["inverse"]
             nc.vector.scalar_tensor_tensor(
-                out=bank["unit"][:, columns].rearrange("p (b i) -> p b i", i=POSITIONS),
-                in0=inverse[:, span].unsqueeze(2).to_broadcast([P, samples, POSITIONS]),
+                out=bank["unit"][:, nodes, :],
+                in0=bank["inverse"][:, nodes, :],
                 scalar=1.0 / floor,
-                in1=bank["cam"][:, columns].rearrange("p (b i) -> p b i", i=POSITIONS),
+                in1=bank["cam"][:].rearrange("p (t r) -> p r t", t=PACK)[:, nodes, :],
                 op0=ALU.min,
                 op1=ALU.mult,
             )
-
-        def turn_units(bank, pairs):
-            if pairs.start == 0:
-                turned = turns.tile([P, PACK, NODES], BF16, name="unit_turned", tag="turn")
-                bank["turned"] = turned
-            for t in pairs:
-                nc.tensor.transpose(bank["turned"][:, t, :], bank["unit"][:, P * t : P * (t + 1)], ident_bf16[:])
-
-        def regroup_units(bank, pairs):
-            nc.scalar.copy(out=bank["unit_grouped"][:], in_=bank["turned"][:].rearrange("p t r -> p r t"))
 
         def quantise_units(bank, pairs):
             codes = keep.tile([P, NODES], U32, name="unit_codes_%s" % bank["label"], align_bytes=64)
             scales = keep.tile([P, NODES], U8, name="unit_scales_%s" % bank["label"], align_bytes=64)
             nc.vector.quantize_mx(
                 out=codes[:].bitcast(FP8X4), scales=scales[:],
-                in_=bank["unit_grouped"][:].rearrange("p r t -> p (r t)"),
+                in_=bank["unit"][:].rearrange("p r t -> p (r t)"),
             )
             units[bank["label"]] = (codes, scales)
 
@@ -242,7 +235,7 @@ def tile_avsl_graph_pa_t_kernel(tc, fmap_low, w_low, fmap_high, w_high, out):
         def plan(step, task, bank, pairs):
             later.setdefault(step, []).append((task, bank, pairs))
 
-        QLAG, MLAG, SLAG = 1, 2, 2
+        QLAG, MLAG, SLAG = 1, 2, 1
         for step in range(len(chunks) + 12):
             if MLAG <= step < len(chunks) + MLAG:
                 done = chunks[step - MLAG]
@@ -252,14 +245,14 @@ def tile_avsl_graph_pa_t_kernel(tc, fmap_low, w_low, fmap_high, w_high, out):
                     tail = bank is chunks[-1]["bank"]
                     whole = pair == HALF_PAIRS - 1
                     at = step + SLAG
-                    plan(at, add_square_sums, bank, range(pair, pair + 1))
                     if tail or whole:
                         pairs = range(pair, pair + 1) if tail else range(HALF_PAIRS)
-                        plan(at, root_norms, bank, pairs)
-                        plan(at + 1, divide_by_norms, bank, pairs)
-                        plan(at + 2, turn_units, bank, pairs)
+                        plan(at, square_maps, bank, pairs)
+                        plan(at + 1, sum_squares, bank, pairs)
                     if whole:
-                        plan(at + 3, regroup_units, bank, None)
+                        for nodes in (slice(0, NODES),):
+                            plan(at + 2, invert_norms, bank, nodes)
+                            plan(at + 3, divide_by_norms, bank, nodes)
                         plan(at + 4, quantise_units, bank, None)
             if step < len(chunks):
                 regroup(chunks[step])
@@ -279,7 +272,7 @@ def tile_avsl_graph_pa_t_kernel(tc, fmap_low, w_low, fmap_high, w_high, out):
         lo = [units["low_%d" % half] for half in range(HALVES)]
         hi = [units["high_%d" % half] for half in range(HALVES)]
 
-        link = links.tile([NODES, NODES], F32)
+        link = turns.tile([NODES, NODES], F32, name="link", tag="turn")
         for half in range(HALVES):
             nc.tensor.matmul_mx(
                 out=link[:],

@@ -31,6 +31,8 @@ CHUNK = SLABS * PAIR_COLUMNS * PACK
 HALVES = SAMPLES * POSITIONS // K_PASS
 HALF_SAMPLES = SAMPLES // HALVES
 HALF_PAIRS = HALF_SAMPLES // PAIR
+TENSOR_SHARE = (4, 6, 8, 10, 12)
+SCALAR_EXTRA = ()
 VECTOR_EXTRA = ()
 RUN = 4
 
@@ -50,6 +52,8 @@ def tile_avsl_graph_pa_t_kernel(tc, fmap_low, w_low, fmap_high, w_high, out):
         stack.enter_context(tc.manual_schedule())
         ident_words = keep.tile([P, P], F32)
         make_identity(nc, ident_words[:])
+        ident_bf16 = keep.tile([P, P], BF16)
+        make_identity(nc, ident_bf16[:])
         same_sample = keep.tile([P, P], F32)
         nc.gpsimd.memset(same_sample[:], 0.0)
         for b in range(PAIR):
@@ -117,7 +121,7 @@ def tile_avsl_graph_pa_t_kernel(tc, fmap_low, w_low, fmap_high, w_high, out):
                         nc.tensor.transpose(
                             turned[:, s, u, :], words[:, start + u : start + pass_words : 2], ident_words[:]
                         )
-                nc.vector.tensor_copy(
+                nc.scalar.copy(
                     out=grouped_words[:, first : first + 2], in_=turned[:].rearrange("p s u r -> p s r u")
                 )
             return grouped
@@ -132,6 +136,18 @@ def tile_avsl_graph_pa_t_kernel(tc, fmap_low, w_low, fmap_high, w_high, out):
             )
             weights[level] = (codes, scales)
 
+        def spread(chunk):
+            source = chunk["raw"][1].rearrange(
+                "p (j yy py xx px) -> p px py j yy xx", j=PACK, yy=SIDE, py=WINDOW, xx=SIDE, px=WINDOW
+            )
+            spread_words = turns.tile([P, WINDOW, POSITIONS, PACK], BF16, name="spread_words", tag="turn")
+            for py in range(WINDOW):
+                nc.tensor.matmul(
+                    spread_words[:, py].rearrange("p (yy xx) j -> p j yy xx", xx=SIDE),
+                    lhsT=ident_bf16[:], rhs=source[:, 0, py], start=True, stop=True,
+                )
+            chunk["spread"] = spread_words
+
         def regroup(chunk):
             grouped = stage.tile([P, CHUNK], BF16, name="grouped", tag="grouped", align_bytes=64)
             for b, copy in enumerate((nc.vector.tensor_copy, nc.scalar.copy)):
@@ -144,9 +160,16 @@ def tile_avsl_graph_pa_t_kernel(tc, fmap_low, w_low, fmap_high, w_high, out):
                         "p (py px b yy xx j) -> p b px yy py j xx",
                         py=WINDOW, px=WINDOW, b=PAIR, yy=SIDE, xx=SIDE, j=PACK,
                     )
-                    for px in range(WINDOW):
-                        if chunk["n"] in VECTOR_EXTRA and b == 1 and px == 0:
+                    for px in (1, 0):
+                        if chunk["n"] in TENSOR_SHARE and b == 1 and px == 0:
+                            nc.scalar.copy(
+                                out=grouped[:].rearrange("p (py px b c) -> p px b py c", py=WINDOW, px=WINDOW, b=PAIR)[:, px, b],
+                                in_=chunk["spread"][:].rearrange("p py i j -> p py (i j)"),
+                            )
+                        elif chunk["n"] in VECTOR_EXTRA and b == 1 and px == 0:
                             nc.vector.tensor_copy(out=target[:, b, px], in_=source[:, px])
+                        elif chunk["n"] in SCALAR_EXTRA and b == 0 and px == 1:
+                            nc.scalar.copy(out=target[:, b, px], in_=source[:, px])
                         else:
                             copy(out=target[:, b, px], in_=source[:, px])
                 else:
@@ -237,18 +260,18 @@ def tile_avsl_graph_pa_t_kernel(tc, fmap_low, w_low, fmap_high, w_high, out):
 
         QLAG, MLAG, SLAG = 1, 2, 1
         for step in range(len(chunks) + 12):
+            if step + 0 in TENSOR_SHARE:
+                spread(chunks[step + 0])
             if MLAG <= step < len(chunks) + MLAG:
                 done = chunks[step - MLAG]
                 multiply_chunk(done)
                 if closes_pair(done):
                     bank, pair = done["bank"], done["pair"]
-                    tail = bank is chunks[-1]["bank"]
                     whole = pair == HALF_PAIRS - 1
                     at = step + SLAG
-                    if tail or whole:
-                        pairs = range(pair, pair + 1) if tail else range(HALF_PAIRS)
-                        plan(at, square_maps, bank, pairs)
-                        plan(at + 1, sum_squares, bank, pairs)
+                    pairs = range(pair, pair + 1)
+                    plan(at, square_maps, bank, pairs)
+                    plan(at + 1, sum_squares, bank, pairs)
                     if whole:
                         for nodes in (slice(0, NODES),):
                             plan(at + 2, invert_norms, bank, nodes)

@@ -31,10 +31,14 @@ CHUNK = SLABS * PAIR_COLUMNS * PACK
 HALVES = SAMPLES * POSITIONS // K_PASS
 HALF_SAMPLES = SAMPLES // HALVES
 HALF_PAIRS = HALF_SAMPLES // PAIR
-TENSOR_SHARE = (4, 6, 8, 10, 12)
-SCALAR_EXTRA = ()
-VECTOR_EXTRA = ()
 RUN = 4
+
+W_LOW_AT = 1
+W_HIGH_AT = 14
+W_HIGH_TURN = 14
+TENSOR_SHARE = (4, 6, 8, 10, 12)
+VECTOR_EXTRA = ()
+FINE_LOADS = 1
 
 FLOPS = 2 * NODES * SAMPLES * (C_LOW * POSITIONS * WINDOW * WINDOW + C_HIGH * POSITIONS + NODES * POSITIONS)
 
@@ -48,8 +52,13 @@ def tile_avsl_graph_pa_t_kernel(tc, fmap_low, w_low, fmap_high, w_high, out):
         quant = stack.enter_context(tc.tile_pool(name="quant", bufs=8))
         cams = stack.enter_context(tc.psum_pool(name="cams", bufs=2 * HALVES))
         turns = stack.enter_context(tc.psum_pool(name="turns", bufs=4))
-
         stack.enter_context(tc.manual_schedule())
+
+        one = keep.tile([P, 1], F32)
+        nc.vector.memset(one[:], 1.0)
+        root_of_one = keep.tile([P, 1], F32)
+        nc.scalar.activation(out=root_of_one[:], in_=one[:], func=ACT.Abs_reciprocal_sqrt)
+
         ident_words = keep.tile([P, P], F32)
         make_identity(nc, ident_words[:])
         ident_bf16 = keep.tile([P, P], BF16)
@@ -60,61 +69,67 @@ def tile_avsl_graph_pa_t_kernel(tc, fmap_low, w_low, fmap_high, w_high, out):
             rows = slice(POSITIONS * b, POSITIONS * (b + 1))
             nc.gpsimd.memset(same_sample[rows, rows], 1.0)
 
-        one = keep.tile([P, 1], F32)
-        nc.vector.memset(one[:], 1.0)
-        root_of_one = keep.tile([P, 1], F32)
-        nc.scalar.activation(out=root_of_one[:], in_=one[:], func=ACT.Abs_reciprocal_sqrt)
-
         w_low_rows = keep.tile([NODES, C_LOW], BF16)
         w_high_rows = keep.tile([NODES, C_HIGH], BF16)
-        banks = {}
+        banks = []
         chunks = []
         for level in ("low", "high"):
             for half in range(HALVES):
-                banks[(level, half)] = {
-                    "label": "%s_%d" % (level, half),
+                label = "%s_%d" % (level, half)
+                last = level == "high" and half == HALVES - 1
+                bank = {
+                    "label": label,
                     "level": level,
-                    "cam": cams.tile([P, K_PASS], F32, name="cam_%s_%d" % (level, half), tag="cam"),
-                    "squares": keep.tile([P, K_PASS], F32, name="squares_%s_%d" % (level, half)),
-                    "inverse": keep.tile([P, NODES, PACK], F32, name="inverse_%s_%d" % (level, half)),
-                    "unit": keep.tile([P, NODES, PACK], BF16, name="unit_%s_%d" % (level, half), align_bytes=64),
+                    "squares": keep.tile([P, K_PASS], F32, name="squares_" + label),
+                    "inverse": keep.tile([P, K_PASS], F32, name="inverse_" + label),
+                    "unit": keep.tile([P, NODES, PACK], BF16, name="unit_" + label, align_bytes=64),
+                    "groups": [],
                 }
-                for pair in range(HALF_PAIRS):
-                    for s in range(LOW_PASSES if level == "low" else 1):
-                        chunks.append({"level": level, "bank": banks[(level, half)], "pair": pair, "s": s, "n": len(chunks), "sample": HALF_SAMPLES * half + PAIR * pair})
-        for n, chunk in enumerate(chunks):
-            if n == 1:
+                for pairs in (range(HALF_PAIRS - 1), range(HALF_PAIRS - 1, HALF_PAIRS)) if last else (range(HALF_PAIRS),):
+                    group = {"bank": bank, "pairs": pairs, "whole": not last}
+                    group["cam"] = cams.tile([P, len(pairs), NODES], F32, name="cam_%s_%d" % (label, pairs.start), tag="cam")
+                    bank["groups"].append(group)
+                    for pair in pairs:
+                        for s in range(LOW_PASSES if level == "low" else 1):
+                            chunks.append({
+                                "level": level, "group": group, "pair": pair, "s": s, "n": len(chunks),
+                                "sample": HALF_SAMPLES * half + PAIR * pair,
+                                "closes": level == "high" or s == LOW_PASSES - 1,
+                            })
+                banks.append(bank)
+
+        for chunk in chunks:
+            n = chunk["n"]
+            if n == W_LOW_AT:
                 nc.sync.dma_start(out=w_low_rows[:], in_=w_low)
-            if n == 8:
+            if n == W_HIGH_AT:
                 nc.sync.dma_start(out=w_high_rows[:], in_=w_high)
             landing = raws.tile([P, PAIR, CHUNK // PAIR], BF16, name="raw_%d" % n, tag="raw")
-            samples = slice(chunk["sample"], chunk["sample"] + PAIR)
-            s = chunk["s"]
-            pieces = [slice(b, b + 1) for b in range(PAIR)] if n in (0,) else [slice(0, PAIR)]
-            for piece in pieces:
-                source = slice(chunk["sample"] + piece.start, chunk["sample"] + piece.stop)
-                if chunk["level"] == "low":
+            chunk["raw"] = landing
+            if chunk["level"] == "low":
+                channels = slice(K_PASS * chunk["s"], K_PASS * (chunk["s"] + 1))
+                step = 1 if n < FINE_LOADS else PAIR
+                for b in range(0, PAIR, step):
+                    samples = slice(chunk["sample"] + b, chunk["sample"] + b + step)
                     nc.sync.dma_start(
-                        out=landing[:, piece],
-                        in_=fmap_low[source, K_PASS * s : K_PASS * (s + 1)].rearrange(
-                            "b (p j) y x -> p b (j y x)", j=PACK
-                        ),
+                        out=landing[:, b : b + step],
+                        in_=fmap_low[samples, channels].rearrange("b (p j) y x -> p b (j y x)", j=PACK),
                     )
-                else:
-                    for b in range(piece.start, piece.stop):
-                        nc.sync.dma_start(
-                            out=landing[:, b].rearrange("p (s e) -> p s e", s=HIGH_PASSES),
-                            in_=fmap_high[chunk["sample"] + b].rearrange("(s p j) y x -> p s (j y x)", s=HIGH_PASSES, j=PACK),
-                        )
-            chunk["raw"] = [landing[:, b, :] for b in range(PAIR)]
+            else:
+                nc.sync.dma_start(
+                    out=landing[:].rearrange("p b (s e) -> p (b s) e", s=HIGH_PASSES),
+                    in_=fmap_high[chunk["sample"] : chunk["sample"] + PAIR].rearrange(
+                        "b (s p j) y x -> p (b s) (j y x)", s=HIGH_PASSES, j=PACK
+                    ),
+                )
 
         def turn_weights(rows, passes, level):
             words = rows[:].bitcast(F32)
             pass_words = K_PASS // 2
-            grouped = keep.tile([P, passes * NODES * PACK], BF16, name="w_grouped_%s" % level, align_bytes=64)
+            grouped = keep.tile([P, passes * NODES * PACK], BF16, name="w_grouped_" + level, align_bytes=64)
             grouped_words = grouped[:].bitcast(F32).rearrange("p (s r u) -> p s r u", r=NODES, u=2)
             for first in range(0, passes, 2):
-                turned = turns.tile([P, 2, 2, NODES], F32, name="w_turned_%s" % level, tag="turn")
+                turned = turns.tile([P, 2, 2, NODES], F32, name="w_turned_" + level, tag="turn")
                 for s in range(2):
                     for u in range(2):
                         start = pass_words * (first + s)
@@ -126,9 +141,9 @@ def tile_avsl_graph_pa_t_kernel(tc, fmap_low, w_low, fmap_high, w_high, out):
                 )
             return grouped
 
-        def quantise_turned_weights(grouped, passes, level):
-            codes = keep.tile([P, passes, NODES], U32, name="w_codes_%s" % level, align_bytes=64)
-            scales = keep.tile([P, passes, NODES], U8, name="w_scales_%s" % level, align_bytes=64)
+        def quantise_weights(grouped, passes, level):
+            codes = keep.tile([P, passes, NODES], U32, name="w_codes_" + level, align_bytes=64)
+            scales = keep.tile([P, passes, NODES], U8, name="w_scales_" + level, align_bytes=64)
             nc.vector.quantize_mx(
                 out=codes[:].rearrange("p s r -> p (s r)").bitcast(FP8X4),
                 scales=scales[:].rearrange("p s r -> p (s r)"),
@@ -137,7 +152,7 @@ def tile_avsl_graph_pa_t_kernel(tc, fmap_low, w_low, fmap_high, w_high, out):
             weights[level] = (codes, scales)
 
         def spread(chunk):
-            source = chunk["raw"][1].rearrange(
+            source = chunk["raw"][:, 1].rearrange(
                 "p (j yy py xx px) -> p px py j yy xx", j=PACK, yy=SIDE, py=WINDOW, xx=SIDE, px=WINDOW
             )
             spread_words = turns.tile([P, WINDOW, POSITIONS, PACK], BF16, name="spread_words", tag="turn")
@@ -148,37 +163,35 @@ def tile_avsl_graph_pa_t_kernel(tc, fmap_low, w_low, fmap_high, w_high, out):
                 )
             chunk["spread"] = spread_words
 
-        def regroup(chunk):
+        def regroup_low(chunk):
             grouped = stage.tile([P, CHUNK], BF16, name="grouped", tag="grouped", align_bytes=64)
-            for b, copy in enumerate((nc.vector.tensor_copy, nc.scalar.copy)):
-                raw = chunk["raw"][b]
-                if chunk["level"] == "low":
-                    source = raw.rearrange(
-                        "p (j yy py xx px) -> p px yy py j xx", j=PACK, yy=SIDE, py=WINDOW, xx=SIDE, px=WINDOW
-                    )
-                    target = grouped[:].rearrange(
-                        "p (py px b yy xx j) -> p b px yy py j xx",
-                        py=WINDOW, px=WINDOW, b=PAIR, yy=SIDE, xx=SIDE, j=PACK,
-                    )
-                    for px in (1, 0):
-                        if chunk["n"] in TENSOR_SHARE and b == 1 and px == 0:
-                            nc.scalar.copy(
-                                out=grouped[:].rearrange("p (py px b c) -> p px b py c", py=WINDOW, px=WINDOW, b=PAIR)[:, px, b],
-                                in_=chunk["spread"][:].rearrange("p py i j -> p py (i j)"),
-                            )
-                        elif chunk["n"] in VECTOR_EXTRA and b == 1 and px == 0:
-                            nc.vector.tensor_copy(out=target[:, b, px], in_=source[:, px])
-                        elif chunk["n"] in SCALAR_EXTRA and b == 0 and px == 1:
-                            nc.scalar.copy(out=target[:, b, px], in_=source[:, px])
-                        else:
-                            copy(out=target[:, b, px], in_=source[:, px])
-                else:
-                    source = raw.rearrange("p (s j c i) -> p s c j i", s=HIGH_PASSES, j=PACK, i=RUN)
-                    target = grouped[:].rearrange(
-                        "p (s b c i j) -> p b s c j i", s=HIGH_PASSES, b=PAIR, i=RUN, j=PACK
-                    )
-                    copy(out=target[:, b], in_=source)
             chunk["grouped"] = grouped
+            n = chunk["n"]
+            target = grouped[:].rearrange(
+                "p (py px b yy xx j) -> p b px yy py j xx", py=WINDOW, px=WINDOW, b=PAIR, yy=SIDE, xx=SIDE, j=PACK
+            )
+            for b in range(PAIR):
+                source = chunk["raw"][:, b].rearrange(
+                    "p (j yy py xx px) -> p px yy py j xx", j=PACK, yy=SIDE, py=WINDOW, xx=SIDE, px=WINDOW
+                )
+                for px in (1, 0):
+                    if b == 1 and px == 0 and n in TENSOR_SHARE:
+                        nc.scalar.copy(
+                            out=grouped[:].rearrange("p (py px b c) -> p px b py c", py=WINDOW, px=WINDOW, b=PAIR)[:, px, b],
+                            in_=chunk["spread"][:].rearrange("p py i j -> p py (i j)"),
+                        )
+                    elif b == 0 or (px == 0 and n in VECTOR_EXTRA):
+                        nc.vector.tensor_copy(out=target[:, b, px], in_=source[:, px])
+                    else:
+                        nc.scalar.copy(out=target[:, b, px], in_=source[:, px])
+
+        def regroup_high(chunk):
+            grouped = stage.tile([P, CHUNK], BF16, name="grouped", tag="grouped", align_bytes=64)
+            chunk["grouped"] = grouped
+            target = grouped[:].rearrange("p (s b c i j) -> p b s c j i", s=HIGH_PASSES, b=PAIR, i=RUN, j=PACK)
+            for b, copy in enumerate((nc.vector.tensor_copy, nc.scalar.copy)):
+                source = chunk["raw"][:, b].rearrange("p (s j c i) -> p s c j i", s=HIGH_PASSES, j=PACK, i=RUN)
+                copy(out=target[:, b], in_=source)
 
         def quantise_chunk(chunk):
             codes = quant.tile([P, SLABS, PAIR_COLUMNS], U32, name="codes", tag="codes", align_bytes=64)
@@ -193,60 +206,69 @@ def tile_avsl_graph_pa_t_kernel(tc, fmap_low, w_low, fmap_high, w_high, out):
         def multiply_chunk(chunk):
             low = chunk["level"] == "low"
             w_codes, w_scales = weights[chunk["level"]]
-            pair = chunk["pair"]
-            codes, scales = chunk["codes"], chunk["scales"]
+            group = chunk["group"]
             for slab in range(SLABS):
                 s = chunk["s"] if low else slab
                 nc.tensor.matmul_mx(
-                    out=chunk["bank"]["cam"][:, PAIR_COLUMNS * pair : PAIR_COLUMNS * (pair + 1)],
-                    lhsT=codes[:, slab, :].bitcast(FP8X4),
-                    lhsT_scale=scales[:, slab, :],
+                    out=group["cam"][:, chunk["pair"] - group["pairs"].start, :],
+                    lhsT=chunk["codes"][:, slab, :].bitcast(FP8X4),
+                    lhsT_scale=chunk["scales"][:, slab, :],
                     rhs=w_codes[:, s, :].bitcast(FP8X4),
                     rhs_scale=w_scales[:, s, :],
                     start=(slab == 0 and chunk["s"] == 0),
-                    stop=(slab == SLABS - 1 and closes_pair(chunk)),
+                    stop=(slab == SLABS - 1 and chunk["closes"]),
                 )
 
-        def closes_pair(chunk):
-            return chunk["level"] == "high" or chunk["s"] == LOW_PASSES - 1
-
-        def square_maps(bank, pairs):
-            columns = slice(NODES * pairs.start, NODES * pairs.stop)
-            nc.scalar.activation(out=bank["squares"][:, columns], in_=bank["cam"][:, columns], func=ACT.Square)
-
-        def sum_squares(bank, pairs):
-            columns = slice(NODES * pairs.start, NODES * pairs.stop)
-            if pairs.start == 0:
-                sums = turns.tile([P, K_PASS], F32, name="sums", tag="turn")
-                bank["sums"] = sums
-            nc.tensor.matmul(
-                bank["sums"][:, columns], lhsT=same_sample[:], rhs=bank["squares"][:, columns], start=True, stop=True
-            )
-
-        def invert_norms(bank, nodes):
+        def square_pair(chunk):
+            group, pair = chunk["group"], chunk["pair"]
             nc.scalar.activation(
-                out=bank["inverse"][:, nodes, :],
-                in_=bank["sums"][:].rearrange("p (t r) -> p r t", t=PACK)[:, nodes, :],
-                func=ACT.Abs_reciprocal_sqrt,
+                out=group["bank"]["squares"][:, NODES * pair : NODES * (pair + 1)],
+                in_=group["cam"][:, pair - group["pairs"].start, :],
+                func=ACT.Square,
             )
 
-        def divide_by_norms(bank, nodes):
+        def sum_pair(chunk):
+            group, pair = chunk["group"], chunk["pair"]
+            if pair == group["pairs"].start:
+                sums = turns.tile([P, len(group["pairs"]), NODES], F32, name="sums", tag="turn")
+                group["sums"] = sums
+            nc.tensor.matmul(
+                group["sums"][:, pair - group["pairs"].start, :],
+                lhsT=same_sample[:],
+                rhs=group["bank"]["squares"][:, NODES * pair : NODES * (pair + 1)],
+                start=True, stop=True,
+            )
+
+        def group_views(group):
+            pairs, bank = group["pairs"], group["bank"]
+            inverse = bank["inverse"][:, NODES * pairs.start : NODES * pairs.stop]
+            if group["whole"]:
+                return inverse.rearrange("p (r t) -> p r t", r=NODES), group["sums"][:].rearrange("p t r -> p r t"), inverse.rearrange("p (r t) -> p r t", r=NODES)
+            return inverse, group["sums"][:].rearrange("p t r -> p (t r)"), inverse.rearrange("p (t r) -> p r t", r=NODES)
+
+        def invert_norms(group):
+            target, source, words = group_views(group)
+            nc.scalar.activation(out=target, in_=source, func=ACT.Abs_reciprocal_sqrt)
+
+        def divide_by_norms(group):
+            target, source, words = group_views(group)
+            pairs, bank = group["pairs"], group["bank"]
             floor = WINDOW * WINDOW * EPS if bank["level"] == "low" else EPS
             nc.vector.scalar_tensor_tensor(
-                out=bank["unit"][:, nodes, :],
-                in0=bank["inverse"][:, nodes, :],
+                out=bank["unit"][:, :, pairs.start : pairs.stop],
+                in0=words,
                 scalar=1.0 / floor,
-                in1=bank["cam"][:].rearrange("p (t r) -> p r t", t=PACK)[:, nodes, :],
+                in1=group["cam"][:].rearrange("p t r -> p r t"),
                 op0=ALU.min,
                 op1=ALU.mult,
             )
 
-        def quantise_units(bank, pairs):
-            codes = keep.tile([P, NODES], U32, name="unit_codes_%s" % bank["label"], align_bytes=64)
-            scales = keep.tile([P, NODES], U8, name="unit_scales_%s" % bank["label"], align_bytes=64)
+        def quantise_units(group):
+            bank = group["bank"]
+            codes = keep.tile([P, NODES], U32, name="unit_codes_" + bank["label"], align_bytes=64)
+            scales = keep.tile([P, NODES], U8, name="unit_scales_" + bank["label"], align_bytes=64)
             nc.vector.quantize_mx(
-                out=codes[:].bitcast(FP8X4), scales=scales[:],
-                in_=bank["unit"][:].rearrange("p r t -> p (r t)"),
+                out=codes[:].bitcast(FP8X4), scales=scales[:], in_=bank["unit"][:].rearrange("p r t -> p (r t)")
             )
             units[bank["label"]] = (codes, scales)
 
@@ -254,55 +276,50 @@ def tile_avsl_graph_pa_t_kernel(tc, fmap_low, w_low, fmap_high, w_high, out):
         units = {}
         turned_weights = {}
         later = {}
-
-        def plan(step, task, bank, pairs):
-            later.setdefault(step, []).append((task, bank, pairs))
-
-        QLAG, MLAG, SLAG = 1, 2, 1
-        for step in range(len(chunks) + 12):
-            if step + 0 in TENSOR_SHARE:
-                spread(chunks[step + 0])
-            if MLAG <= step < len(chunks) + MLAG:
-                done = chunks[step - MLAG]
+        M_LAG, S_LAG = 2, 1
+        for step in range(len(chunks) + 9):
+            if step in TENSOR_SHARE:
+                spread(chunks[step])
+            if M_LAG <= step < len(chunks) + M_LAG:
+                done = chunks[step - M_LAG]
                 multiply_chunk(done)
-                if closes_pair(done):
-                    bank, pair = done["bank"], done["pair"]
-                    whole = pair == HALF_PAIRS - 1
-                    at = step + SLAG
-                    pairs = range(pair, pair + 1)
-                    plan(at, square_maps, bank, pairs)
-                    plan(at + 1, sum_squares, bank, pairs)
-                    if whole:
-                        for nodes in (slice(0, NODES),):
-                            plan(at + 2, invert_norms, bank, nodes)
-                            plan(at + 3, divide_by_norms, bank, nodes)
-                        plan(at + 4, quantise_units, bank, None)
+                if done["closes"]:
+                    later.setdefault(step + S_LAG, []).append((square_pair, done))
+                    later.setdefault(step + S_LAG + 1, []).append((sum_pair, done))
+                    group = done["group"]
+                    if done["pair"] == group["pairs"].stop - 1:
+                        later.setdefault(step + S_LAG + 2, []).append((invert_norms, group))
+                        later.setdefault(step + S_LAG + 3, []).append((divide_by_norms, group))
+                        if done["pair"] == HALF_PAIRS - 1:
+                            later.setdefault(step + S_LAG + 4, []).append((quantise_units, group))
             if step < len(chunks):
-                regroup(chunks[step])
+                chunk = chunks[step]
+                if chunk["level"] == "low":
+                    regroup_low(chunk)
+                else:
+                    regroup_high(chunk)
             if step == 0:
                 turned_weights["low"] = turn_weights(w_low_rows, LOW_PASSES, "low")
             if step == 1:
-                quantise_turned_weights(turned_weights["low"], LOW_PASSES, "low")
-            if step == 10:
+                quantise_weights(turned_weights["low"], LOW_PASSES, "low")
+            if step == W_HIGH_TURN:
                 turned_weights["high"] = turn_weights(w_high_rows, HIGH_PASSES, "high")
-            if step == 11:
-                quantise_turned_weights(turned_weights["high"], HIGH_PASSES, "high")
-            if QLAG <= step < len(chunks) + QLAG:
-                quantise_chunk(chunks[step - QLAG])
-            for task, bank, pairs in later.pop(step, []):
-                task(bank, pairs)
-
-        lo = [units["low_%d" % half] for half in range(HALVES)]
-        hi = [units["high_%d" % half] for half in range(HALVES)]
+            if step == W_HIGH_TURN + 1:
+                quantise_weights(turned_weights["high"], HIGH_PASSES, "high")
+            if 1 <= step <= len(chunks):
+                quantise_chunk(chunks[step - 1])
+            for task, subject in later.pop(step, []):
+                task(subject)
 
         link = turns.tile([NODES, NODES], F32, name="link", tag="turn")
         for half in range(HALVES):
+            lo, hi = units["low_%d" % half], units["high_%d" % half]
             nc.tensor.matmul_mx(
                 out=link[:],
-                lhsT=lo[half][0][:].bitcast(FP8X4),
-                lhsT_scale=lo[half][1][:],
-                rhs=hi[half][0][:].bitcast(FP8X4),
-                rhs_scale=hi[half][1][:],
+                lhsT=lo[0][:].bitcast(FP8X4),
+                lhsT_scale=lo[1][:],
+                rhs=hi[0][:].bitcast(FP8X4),
+                rhs_scale=hi[1][:],
                 start=(half == 0),
                 stop=(half == HALVES - 1),
             )

@@ -36,9 +36,9 @@ RUN = 4
 W_LOW_AT = 1
 W_HIGH_AT = 14
 W_HIGH_TURN = 14
-TENSOR_SHARE = (4, 6, 8, 10, 12)
-VECTOR_EXTRA = ()
-FINE_LOADS = 1
+TENSOR_SHARE = (11, 23)
+SPARE_VECTOR = (0,)
+FINE_LOADS = 2
 
 FLOPS = 2 * NODES * SAMPLES * (C_LOW * POSITIONS * WINDOW * WINDOW + C_HIGH * POSITIONS + NODES * POSITIONS)
 
@@ -151,47 +151,44 @@ def tile_avsl_graph_pa_t_kernel(tc, fmap_low, w_low, fmap_high, w_high, out):
             )
             weights[level] = (codes, scales)
 
+        def window_place(chunk, b, px):
+            return chunk["raw"][:, b].rearrange(
+                "p (j yy py xx px) -> p px yy py j xx", j=PACK, yy=SIDE, py=WINDOW, xx=SIDE, px=WINDOW
+            )[:, px]
+
+        def two_passes(chunk, b, h):
+            return chunk["raw"][:, b].rearrange("p (s j i) -> p s j i", s=HIGH_PASSES, j=PACK)[:, 2 * h : 2 * h + 2]
+
         def spread(chunk):
-            source = chunk["raw"][:, 1].rearrange(
-                "p (j yy py xx px) -> p px py j yy xx", j=PACK, yy=SIDE, py=WINDOW, xx=SIDE, px=WINDOW
-            )
-            spread_words = turns.tile([P, WINDOW, POSITIONS, PACK], BF16, name="spread_words", tag="turn")
-            for py in range(WINDOW):
-                nc.tensor.matmul(
-                    spread_words[:, py].rearrange("p (yy xx) j -> p j yy xx", xx=SIDE),
-                    lhsT=ident_bf16[:], rhs=source[:, 0, py], start=True, stop=True,
-                )
+            spread_words = turns.tile([P, 2, PAIR, POSITIONS, PACK], BF16, name="spread_words", tag="turn")
+            for m in range(2):
+                for b in range(PAIR):
+                    target = spread_words[:, m, b]
+                    if chunk["level"] == "low":
+                        source = window_place(chunk, b, 1).rearrange("p yy py j xx -> p py j yy xx")[:, m]
+                        target = target.rearrange("p (yy xx) j -> p j yy xx", xx=SIDE)
+                    else:
+                        source = two_passes(chunk, b, 1)[:, m]
+                        target = target.rearrange("p i j -> p j i")
+                    nc.tensor.matmul(target, lhsT=ident_bf16[:], rhs=source, start=True, stop=True)
             chunk["spread"] = spread_words
 
-        def regroup_low(chunk):
+        def regroup(chunk):
             grouped = stage.tile([P, CHUNK], BF16, name="grouped", tag="grouped", align_bytes=64)
             chunk["grouped"] = grouped
-            n = chunk["n"]
-            target = grouped[:].rearrange(
-                "p (py px b yy xx j) -> p b px yy py j xx", py=WINDOW, px=WINDOW, b=PAIR, yy=SIDE, xx=SIDE, j=PACK
-            )
-            for b in range(PAIR):
-                source = chunk["raw"][:, b].rearrange(
-                    "p (j yy py xx px) -> p px yy py j xx", j=PACK, yy=SIDE, py=WINDOW, xx=SIDE, px=WINDOW
-                )
-                for px in (1, 0):
-                    if b == 1 and px == 0 and n in TENSOR_SHARE:
-                        nc.scalar.copy(
-                            out=grouped[:].rearrange("p (py px b c) -> p px b py c", py=WINDOW, px=WINDOW, b=PAIR)[:, px, b],
-                            in_=chunk["spread"][:].rearrange("p py i j -> p py (i j)"),
-                        )
-                    elif b == 0 or (px == 0 and n in VECTOR_EXTRA):
-                        nc.vector.tensor_copy(out=target[:, b, px], in_=source[:, px])
+            for h, copy in enumerate((nc.vector.tensor_copy, nc.scalar.copy)):
+                half = grouped[:, CHUNK // 2 * h : CHUNK // 2 * (h + 1)]
+                if h == 1 and chunk["n"] in TENSOR_SHARE:
+                    copy(out=half, in_=chunk["spread"][:].rearrange("p m b i j -> p (m b i j)"))
+                    continue
+                for b in range(PAIR):
+                    if chunk["level"] == "low":
+                        target = half.rearrange("p (py b yy xx j) -> p b yy py j xx", py=WINDOW, b=PAIR, yy=SIDE, xx=SIDE)
+                        source = window_place(chunk, b, h)
                     else:
-                        nc.scalar.copy(out=target[:, b, px], in_=source[:, px])
-
-        def regroup_high(chunk):
-            grouped = stage.tile([P, CHUNK], BF16, name="grouped", tag="grouped", align_bytes=64)
-            chunk["grouped"] = grouped
-            target = grouped[:].rearrange("p (s b c i j) -> p b s c j i", s=HIGH_PASSES, b=PAIR, i=RUN, j=PACK)
-            for b, copy in enumerate((nc.vector.tensor_copy, nc.scalar.copy)):
-                source = chunk["raw"][:, b].rearrange("p (s j c i) -> p s c j i", s=HIGH_PASSES, j=PACK, i=RUN)
-                copy(out=target[:, b], in_=source)
+                        target = half.rearrange("p (s b c i j) -> p b s c j i", s=2, b=PAIR, i=RUN, j=PACK)
+                        source = two_passes(chunk, b, h).rearrange("p s j (c i) -> p s c j i", i=RUN)
+                    (nc.vector.tensor_copy if chunk["n"] in SPARE_VECTOR and b == 0 else copy)(out=target[:, b], in_=source)
 
         def quantise_chunk(chunk):
             codes = quant.tile([P, SLABS, PAIR_COLUMNS], U32, name="codes", tag="codes", align_bytes=64)
@@ -276,12 +273,12 @@ def tile_avsl_graph_pa_t_kernel(tc, fmap_low, w_low, fmap_high, w_high, out):
         units = {}
         turned_weights = {}
         later = {}
+        FIRST_MULTIPLY = 2
         M_LAG, S_LAG = 2, 1
         for step in range(len(chunks) + 9):
             if step in TENSOR_SHARE:
                 spread(chunks[step])
-            if M_LAG <= step < len(chunks) + M_LAG:
-                done = chunks[step - M_LAG]
+            for done in [chunk for chunk in chunks if max(chunk["n"] + M_LAG, FIRST_MULTIPLY) == step]:
                 multiply_chunk(done)
                 if done["closes"]:
                     later.setdefault(step + S_LAG, []).append((square_pair, done))
@@ -293,18 +290,14 @@ def tile_avsl_graph_pa_t_kernel(tc, fmap_low, w_low, fmap_high, w_high, out):
                         if done["pair"] == HALF_PAIRS - 1:
                             later.setdefault(step + S_LAG + 4, []).append((quantise_units, group))
             if step < len(chunks):
-                chunk = chunks[step]
-                if chunk["level"] == "low":
-                    regroup_low(chunk)
-                else:
-                    regroup_high(chunk)
+                regroup(chunks[step])
             if step == 0:
                 turned_weights["low"] = turn_weights(w_low_rows, LOW_PASSES, "low")
             if step == 1:
                 quantise_weights(turned_weights["low"], LOW_PASSES, "low")
             if step == W_HIGH_TURN:
                 turned_weights["high"] = turn_weights(w_high_rows, HIGH_PASSES, "high")
-            if step == W_HIGH_TURN + 1:
+            if step == W_HIGH_TURN + 2:
                 quantise_weights(turned_weights["high"], HIGH_PASSES, "high")
             if 1 <= step <= len(chunks):
                 quantise_chunk(chunks[step - 1])

@@ -33,12 +33,12 @@ HALF_SAMPLES = SAMPLES // HALVES
 HALF_PAIRS = HALF_SAMPLES // PAIR
 RUN = 4
 
-W_LOW_AT = 1
+W_LOW_AT = 2
 W_HIGH_AT = 14
 W_HIGH_TURN = 14
-TENSOR_SHARE = (11, 23)
+TENSOR_SHARE = (17, 23)
 SPARE_VECTOR = (0,)
-FINE_LOADS = 2
+FINE_LOADS = 3
 
 FLOPS = 2 * NODES * SAMPLES * (C_LOW * POSITIONS * WINDOW * WINDOW + C_HIGH * POSITIONS + NODES * POSITIONS)
 
@@ -85,7 +85,7 @@ def tile_avsl_graph_pa_t_kernel(tc, fmap_low, w_low, fmap_high, w_high, out):
                     "unit": keep.tile([P, NODES, PACK], BF16, name="unit_" + label, align_bytes=64),
                     "groups": [],
                 }
-                for pairs in (range(HALF_PAIRS - 1), range(HALF_PAIRS - 1, HALF_PAIRS)) if last else (range(HALF_PAIRS),):
+                for pairs in (range(2), range(2, 3), range(3, 4)) if last else (range(HALF_PAIRS),):
                     group = {"bank": bank, "pairs": pairs, "whole": not last}
                     group["cam"] = cams.tile([P, len(pairs), NODES], F32, name="cam_%s_%d" % (label, pairs.start), tag="cam")
                     bank["groups"].append(group)
@@ -193,11 +193,15 @@ def tile_avsl_graph_pa_t_kernel(tc, fmap_low, w_low, fmap_high, w_high, out):
         def quantise_chunk(chunk):
             codes = quant.tile([P, SLABS, PAIR_COLUMNS], U32, name="codes", tag="codes", align_bytes=64)
             scales = quant.tile([P, SLABS, PAIR_COLUMNS], U8, name="scales", tag="scales", align_bytes=64)
-            nc.vector.quantize_mx(
-                out=codes[:].rearrange("p m c -> p (m c)").bitcast(FP8X4),
-                scales=scales[:].rearrange("p m c -> p (m c)"),
-                in_=chunk["grouped"][:],
-            )
+            parts = 2 if chunk is chunks[-1] else 1
+            for part in range(parts):
+                slabs = slice(SLABS * part // parts, SLABS * (part + 1) // parts)
+                values = slice(CHUNK * part // parts, CHUNK * (part + 1) // parts)
+                nc.vector.quantize_mx(
+                    out=codes[:, slabs].rearrange("p m c -> p (m c)").bitcast(FP8X4),
+                    scales=scales[:, slabs].rearrange("p m c -> p (m c)"),
+                    in_=chunk["grouped"][:, values],
+                )
             chunk["codes"], chunk["scales"] = codes, scales
 
         def multiply_chunk(chunk):
@@ -273,11 +277,11 @@ def tile_avsl_graph_pa_t_kernel(tc, fmap_low, w_low, fmap_high, w_high, out):
         units = {}
         turned_weights = {}
         later = {}
-        FIRST_MULTIPLY = 2
+        FIRST_MULTIPLY = 4
         M_LAG, S_LAG = 2, 1
-        for step in range(len(chunks) + 9):
-            if step in TENSOR_SHARE:
-                spread(chunks[step])
+        for step in range(len(chunks) + 1):
+            if step + 1 in TENSOR_SHARE:
+                spread(chunks[step + 1])
             for done in [chunk for chunk in chunks if max(chunk["n"] + M_LAG, FIRST_MULTIPLY) == step]:
                 multiply_chunk(done)
                 if done["closes"]:
@@ -291,9 +295,9 @@ def tile_avsl_graph_pa_t_kernel(tc, fmap_low, w_low, fmap_high, w_high, out):
                             later.setdefault(step + S_LAG + 4, []).append((quantise_units, group))
             if step < len(chunks):
                 regroup(chunks[step])
-            if step == 0:
+            if step == 2:
                 turned_weights["low"] = turn_weights(w_low_rows, LOW_PASSES, "low")
-            if step == 1:
+            if step == 3:
                 quantise_weights(turned_weights["low"], LOW_PASSES, "low")
             if step == W_HIGH_TURN:
                 turned_weights["high"] = turn_weights(w_high_rows, HIGH_PASSES, "high")
@@ -301,8 +305,33 @@ def tile_avsl_graph_pa_t_kernel(tc, fmap_low, w_low, fmap_high, w_high, out):
                 quantise_weights(turned_weights["high"], HIGH_PASSES, "high")
             if 1 <= step <= len(chunks):
                 quantise_chunk(chunks[step - 1])
-            for task, subject in later.pop(step, []):
+            for task, subject in later.pop(step, []) if step < len(chunks) else ():
                 task(subject)
+
+        before, last = chunks[-2:]
+        first_group, second_group, third_group = last["group"]["bank"]["groups"]
+        other = chunks[-HALF_PAIRS - 1]["group"]
+        for task, subject in (
+            (square_pair, chunks[-3]),
+            (sum_pair, chunks[-4]),
+            (invert_norms, other),
+            (multiply_chunk, last),
+            (square_pair, before),
+            (sum_pair, chunks[-3]),
+            (divide_by_norms, other),
+            (quantise_units, other),
+            (square_pair, last),
+            (sum_pair, before),
+            (invert_norms, first_group),
+            (divide_by_norms, first_group),
+            (sum_pair, last),
+            (invert_norms, second_group),
+            (divide_by_norms, second_group),
+            (invert_norms, third_group),
+            (divide_by_norms, third_group),
+            (quantise_units, third_group),
+        ):
+            task(subject)
 
         link = turns.tile([NODES, NODES], F32, name="link", tag="turn")
         for half in range(HALVES):

@@ -50,8 +50,8 @@ def tile_avsl_graph_pa_t_kernel(tc, fmap_low, w_low, fmap_high, w_high, out):
         raws = stack.enter_context(tc.tile_pool(name="raws", bufs=(LOW_PASSES + 1) * SAMPLES // PAIR))
         stage = stack.enter_context(tc.tile_pool(name="stage", bufs=6))
         quant = stack.enter_context(tc.tile_pool(name="quant", bufs=8))
-        cams = stack.enter_context(tc.psum_pool(name="cams", bufs=2 * HALVES))
-        turns = stack.enter_context(tc.psum_pool(name="turns", bufs=4))
+        cams = stack.enter_context(tc.psum_pool(name="cams", bufs=5))
+        turns = stack.enter_context(tc.psum_pool(name="turns", bufs=3))
         stack.enter_context(tc.manual_schedule())
 
         one = keep.tile([P, 1], F32)
@@ -280,19 +280,19 @@ def tile_avsl_graph_pa_t_kernel(tc, fmap_low, w_low, fmap_high, w_high, out):
         FIRST_MULTIPLY = 4
         M_LAG, S_LAG = 2, 1
         for step in range(len(chunks) + 1):
-            if step + 1 in TENSOR_SHARE:
-                spread(chunks[step + 1])
             for done in [chunk for chunk in chunks if max(chunk["n"] + M_LAG, FIRST_MULTIPLY) == step]:
                 multiply_chunk(done)
                 if done["closes"]:
                     later.setdefault(step + S_LAG, []).append((square_pair, done))
                     later.setdefault(step + S_LAG + 1, []).append((sum_pair, done))
                     group = done["group"]
-                    if done["pair"] == group["pairs"].stop - 1:
+                    if done["pair"] == group["pairs"].stop - 1 and group["bank"] is not banks[HALVES - 1]:
                         later.setdefault(step + S_LAG + 2, []).append((invert_norms, group))
                         later.setdefault(step + S_LAG + 3, []).append((divide_by_norms, group))
                         if done["pair"] == HALF_PAIRS - 1:
                             later.setdefault(step + S_LAG + 4, []).append((quantise_units, group))
+            if step + 1 in TENSOR_SHARE:
+                spread(chunks[step + 1])
             if step < len(chunks):
                 regroup(chunks[step])
             if step == 2:
@@ -311,19 +311,23 @@ def tile_avsl_graph_pa_t_kernel(tc, fmap_low, w_low, fmap_high, w_high, out):
         before, last = chunks[-2:]
         first_group, second_group, third_group = last["group"]["bank"]["groups"]
         other = chunks[-HALF_PAIRS - 1]["group"]
+        low = banks[HALVES - 1]["groups"][0]
         for task, subject in (
             (square_pair, chunks[-3]),
             (sum_pair, chunks[-4]),
             (invert_norms, other),
+            (invert_norms, low),
             (multiply_chunk, last),
             (square_pair, before),
             (sum_pair, chunks[-3]),
             (divide_by_norms, other),
+            (divide_by_norms, low),
             (quantise_units, other),
             (square_pair, last),
             (sum_pair, before),
             (invert_norms, first_group),
             (divide_by_norms, first_group),
+            (quantise_units, low),
             (sum_pair, last),
             (invert_norms, second_group),
             (divide_by_norms, second_group),

from contextlib import ExitStack

import concourse.mybir as mybir
from concourse.masks import make_identity

BF16 = mybir.dt.bfloat16
F32 = mybir.dt.float32
U32 = mybir.dt.uint32
U8 = mybir.dt.uint8
FP8X4 = mybir.dt.float8_e4m3fn_x4
ACT = mybir.ActivationFunctionType
ALU = mybir.AluOpType

P = 128
PACK = 4
K_PASS = P * PACK

SAMPLES = 16
NODES = 128
C_LOW, C_HIGH = 1024, 2048
LOW_PASSES, HIGH_PASSES = C_LOW // K_PASS, C_HIGH // K_PASS
SIDE = 8
WINDOW = 2
POSITIONS = SIDE * SIDE
EPS = 1e-12

PAIR = 2
PAIR_COLUMNS = PAIR * POSITIONS
SLABS = 4
CHUNK = SLABS * PAIR_COLUMNS * PACK
HALVES = SAMPLES * POSITIONS // K_PASS
HALF_SAMPLES = SAMPLES // HALVES
HALF_PAIRS = HALF_SAMPLES // PAIR
RUN = 4

W_LOW_AT = 2
W_HIGH_AT = 14
W_HIGH_TURN = 14
TENSOR_SHARE = (17, 23)
SPARE_VECTOR = (0,)
FINE_LOADS = 3

FLOPS = 2 * NODES * SAMPLES * (C_LOW * POSITIONS * WINDOW * WINDOW + C_HIGH * POSITIONS + NODES * POSITIONS)


def tile_avsl_graph_pa_t_kernel(tc, fmap_low, w_low, fmap_high, w_high, out):
    nc = tc.nc
    with ExitStack() as stack:
        keep = stack.enter_context(tc.tile_pool(name="keep", bufs=1))
        raws = stack.enter_context(tc.tile_pool(name="raws", bufs=(LOW_PASSES + 1) * SAMPLES // PAIR))
        stage = stack.enter_context(tc.tile_pool(name="stage", bufs=6))
        quant = stack.enter_context(tc.tile_pool(name="quant", bufs=8))
        cams = stack.enter_context(tc.psum_pool(name="cams", bufs=5))
        turns = stack.enter_context(tc.psum_pool(name="turns", bufs=3))
        stack.enter_context(tc.manual_schedule())

        one = keep.tile([P, 1], F32)
        nc.vector.memset(one[:], 1.0)
        root_of_one = keep.tile([P, 1], F32)
        nc.scalar.activation(out=root_of_one[:], in_=one[:], func=ACT.Abs_reciprocal_sqrt)

        ident_words = keep.tile([P, P], F32)
        make_identity(nc, ident_words[:])
        ident_bf16 = keep.tile([P, P], BF16)
        make_identity(nc, ident_bf16[:])
        same_sample = keep.tile([P, P], F32)
        nc.gpsimd.memset(same_sample[:], 0.0)
        for b in range(PAIR):
            rows = slice(POSITIONS * b, POSITIONS * (b + 1))
            nc.gpsimd.memset(same_sample[rows, rows], 1.0)

        w_low_rows = keep.tile([NODES, C_LOW], BF16)
        w_high_rows = keep.tile([NODES, C_HIGH], BF16)
        banks = []
        chunks = []
        for level in ("low", "high"):
            for half in range(HALVES):
                label = "%s_%d" % (level, half)
                last = level == "high" and half == HALVES - 1
                bank = {
                    "label": label,
                    "level": level,
                    "squares": keep.tile([P, K_PASS], F32, name="squares_" + label),
                    "inverse": keep.tile([P, K_PASS], F32, name="inverse_" + label),
                    "unit": keep.tile([P, NODES, PACK], BF16, name="unit_" + label, align_bytes=64),
                    "groups": [],
                }
                for pairs in (range(2), range(2, 3), range(3, 4)) if last else (range(HALF_PAIRS),):
                    group = {"bank": bank, "pairs": pairs, "whole": not last}
                    group["cam"] = cams.tile([P, len(pairs), NODES], F32, name="cam_%s_%d" % (label, pairs.start), tag="cam")
                    bank["groups"].append(group)
                    for pair in pairs:
                        for s in range(LOW_PASSES if level == "low" else 1):
                            chunks.append({
                                "level": level, "group": group, "pair": pair, "s": s, "n": len(chunks),
                                "sample": HALF_SAMPLES * half + PAIR * pair,
                                "closes": level == "high" or s == LOW_PASSES - 1,
                            })
                banks.append(bank)

        for chunk in chunks:
            n = chunk["n"]
            if n == W_LOW_AT:
                nc.sync.dma_start(out=w_low_rows[:], in_=w_low)
            if n == W_HIGH_AT:
                nc.sync.dma_start(out=w_high_rows[:], in_=w_high)
            landing = raws.tile([P, PAIR, CHUNK // PAIR], BF16, name="raw_%d" % n, tag="raw")
            chunk["raw"] = landing
            if chunk["level"] == "low":
                channels = slice(K_PASS * chunk["s"], K_PASS * (chunk["s"] + 1))
                step = 1 if n < FINE_LOADS else PAIR
                for b in range(0, PAIR, step):
                    samples = slice(chunk["sample"] + b, chunk["sample"] + b + step)
                    nc.sync.dma_start(
                        out=landing[:, b : b + step],
                        in_=fmap_low[samples, channels].rearrange("b (p j) y x -> p b (j y x)", j=PACK),
                    )
            else:
                nc.sync.dma_start(
                    out=landing[:].rearrange("p b (s e) -> p (b s) e", s=HIGH_PASSES),
                    in_=fmap_high[chunk["sample"] : chunk["sample"] + PAIR].rearrange(
                        "b (s p j) y x -> p (b s) (j y x)", s=HIGH_PASSES, j=PACK
                    ),
                )

        def turn_weights(rows, passes, level):
            words = rows[:].bitcast(F32)
            pass_words = K_PASS // 2
            grouped = keep.tile([P, passes * NODES * PACK], BF16, name="w_grouped_" + level, align_bytes=64)
            grouped_words = grouped[:].bitcast(F32).rearrange("p (s r u) -> p s r u", r=NODES, u=2)
            for first in range(0, passes, 2):
                turned = turns.tile([P, 2, 2, NODES], F32, name="w_turned_" + level, tag="turn")
                for s in range(2):
                    for u in range(2):
                        start = pass_words * (first + s)
                        nc.tensor.transpose(
                            turned[:, s, u, :], words[:, start + u : start + pass_words : 2], ident_words[:]
                        )
                nc.scalar.copy(
                    out=grouped_words[:, first : first + 2], in_=turned[:].rearrange("p s u r -> p s r u")
                )
            return grouped

        def quantise_weights(grouped, passes, level):
            codes = keep.tile([P, passes, NODES], U32, name="w_codes_" + level, align_bytes=64)
            scales = keep.tile([P, passes, NODES], U8, name="w_scales_" + level, align_bytes=64)
            nc.vector.quantize_mx(
                out=codes[:].rearrange("p s r -> p (s r)").bitcast(FP8X4),
                scales=scales[:].rearrange("p s r -> p (s r)"),
                in_=grouped[:],
            )
            weights[level] = (codes, scales)

        def window_place(chunk, b, px):
            return chunk["raw"][:, b].rearrange(
                "p (j yy py xx px) -> p px yy py j xx", j=PACK, yy=SIDE, py=WINDOW, xx=SIDE, px=WINDOW
            )[:, px]

        def two_passes(chunk, b, h):
            return chunk["raw"][:, b].rearrange("p (s j i) -> p s j i", s=HIGH_PASSES, j=PACK)[:, 2 * h : 2 * h + 2]

        def spread(chunk):
            spread_words = turns.tile([P, 2, PAIR, POSITIONS, PACK], BF16, name="spread_words", tag="turn")
            for m in range(2):
                for b in range(PAIR):
                    target = spread_words[:, m, b]
                    if chunk["level"] == "low":
                        source = window_place(chunk, b, 1).rearrange("p yy py j xx -> p py j yy xx")[:, m]
                        target = target.rearrange("p (yy xx) j -> p j yy xx", xx=SIDE)
                    else:
                        source = two_passes(chunk, b, 1)[:, m]
                        target = target.rearrange("p i j -> p j i")
                    nc.tensor.matmul(target, lhsT=ident_bf16[:], rhs=source, start=True, stop=True)
            chunk["spread"] = spread_words

        def regroup(chunk):
            grouped = stage.tile([P, CHUNK], BF16, name="grouped", tag="grouped", align_bytes=64)
            chunk["grouped"] = grouped
            for h, copy in enumerate((nc.vector.tensor_copy, nc.scalar.copy)):
                half = grouped[:, CHUNK // 2 * h : CHUNK // 2 * (h + 1)]
                if h == 1 and chunk["n"] in TENSOR_SHARE:
                    copy(out=half, in_=chunk["spread"][:].rearrange("p m b i j -> p (m b i j)"))
                    continue
                for b in range(PAIR):
                    if chunk["level"] == "low":
                        target = half.rearrange("p (py b yy xx j) -> p b yy py j xx", py=WINDOW, b=PAIR, yy=SIDE, xx=SIDE)
                        source = window_place(chunk, b, h)
                    else:
                        target = half.rearrange("p (s b c i j) -> p b s c j i", s=2, b=PAIR, i=RUN, j=PACK)
                        source = two_passes(chunk, b, h).rearrange("p s j (c i) -> p s c j i", i=RUN)
                    (nc.vector.tensor_copy if chunk["n"] in SPARE_VECTOR and b == 0 else copy)(out=target[:, b], in_=source)

        def quantise_chunk(chunk):
            codes = quant.tile([P, SLABS, PAIR_COLUMNS], U32, name="codes", tag="codes", align_bytes=64)
            scales = quant.tile([P, SLABS, PAIR_COLUMNS], U8, name="scales", tag="scales", align_bytes=64)
            parts = 2 if chunk is chunks[-1] else 1
            for part in range(parts):
                slabs = slice(SLABS * part // parts, SLABS * (part + 1) // parts)
                values = slice(CHUNK * part // parts, CHUNK * (part + 1) // parts)
                nc.vector.quantize_mx(
                    out=codes[:, slabs].rearrange("p m c -> p (m c)").bitcast(FP8X4),
                    scales=scales[:, slabs].rearrange("p m c -> p (m c)"),
                    in_=chunk["grouped"][:, values],
                )
            chunk["codes"], chunk["scales"] = codes, scales

        def multiply_chunk(chunk):
            low = chunk["level"] == "low"
            w_codes, w_scales = weights[chunk["level"]]
            group = chunk["group"]
            for slab in range(SLABS):
                s = chunk["s"] if low else slab
                nc.tensor.matmul_mx(
                    out=group["cam"][:, chunk["pair"] - group["pairs"].start, :],
                    lhsT=chunk["codes"][:, slab, :].bitcast(FP8X4),
                    lhsT_scale=chunk["scales"][:, slab, :],
                    rhs=w_codes[:, s, :].bitcast(FP8X4),
                    rhs_scale=w_scales[:, s, :],
                    start=(slab == 0 and chunk["s"] == 0),
                    stop=(slab == SLABS - 1 and chunk["closes"]),
                )

        def square_pair(chunk):
            group, pair = chunk["group"], chunk["pair"]
            nc.scalar.activation(
                out=group["bank"]["squares"][:, NODES * pair : NODES * (pair + 1)],
                in_=group["cam"][:, pair - group["pairs"].start, :],
                func=ACT.Square,
            )

        def sum_pair(chunk):
            group, pair = chunk["group"], chunk["pair"]
            if pair == group["pairs"].start:
                sums = turns.tile([P, len(group["pairs"]), NODES], F32, name="sums", tag="turn")
                group["sums"] = sums
            nc.tensor.matmul(
                group["sums"][:, pair - group["pairs"].start, :],
                lhsT=same_sample[:],
                rhs=group["bank"]["squares"][:, NODES * pair : NODES * (pair + 1)],
                start=True, stop=True,
            )

        def group_views(group):
            pairs, bank = group["pairs"], group["bank"]
            inverse = bank["inverse"][:, NODES * pairs.start : NODES * pairs.stop]
            if group["whole"]:
                return inverse.rearrange("p (r t) -> p r t", r=NODES), group["sums"][:].rearrange("p t r -> p r t"), inverse.rearrange("p (r t) -> p r t", r=NODES)
            return inverse, group["sums"][:].rearrange("p t r -> p (t r)"), inverse.rearrange("p (t r) -> p r t", r=NODES)

        def invert_norms(group):
            target, source, words = group_views(group)
            nc.scalar.activation(out=target, in_=source, func=ACT.Abs_reciprocal_sqrt)

        def divide_by_norms(group):
            target, source, words = group_views(group)
            pairs, bank = group["pairs"], group["bank"]
            floor = WINDOW * WINDOW * EPS if bank["level"] == "low" else EPS
            nc.vector.scalar_tensor_tensor(
                out=bank["unit"][:, :, pairs.start : pairs.stop],
                in0=words,
                scalar=1.0 / floor,
                in1=group["cam"][:].rearrange("p t r -> p r t"),
                op0=ALU.min,
                op1=ALU.mult,
            )

        def quantise_units(group):
            bank = group["bank"]
            codes = keep.tile([P, NODES], U32, name="unit_codes_" + bank["label"], align_bytes=64)
            scales = keep.tile([P, NODES], U8, name="unit_scales_" + bank["label"], align_bytes=64)
            nc.vector.quantize_mx(
                out=codes[:].bitcast(FP8X4), scales=scales[:], in_=bank["unit"][:].rearrange("p r t -> p (r t)")
            )
            units[bank["label"]] = (codes, scales)

        weights = {}
        units = {}
        turned_weights = {}
        later = {}
        FIRST_MULTIPLY = 4
        M_LAG, S_LAG = 2, 1
        for step in range(len(chunks) + 1):
            for done in [chunk for chunk in chunks if max(chunk["n"] + M_LAG, FIRST_MULTIPLY) == step]:
                multiply_chunk(done)
                if done["closes"]:
                    later.setdefault(step + S_LAG, []).append((square_pair, done))
                    later.setdefault(step + S_LAG + 1, []).append((sum_pair, done))
                    group = done["group"]
                    if done["pair"] == group["pairs"].stop - 1 and group["bank"] is not banks[HALVES - 1]:
                        later.setdefault(step + S_LAG + 2, []).append((invert_norms, group))
                        later.setdefault(step + S_LAG + 3, []).append((divide_by_norms, group))
                        if done["pair"] == HALF_PAIRS - 1:
                            later.setdefault(step + S_LAG + 4, []).append((quantise_units, group))
            if step + 1 in TENSOR_SHARE:
                spread(chunks[step + 1])
            if step < len(chunks):
                regroup(chunks[step])
            if step == 2:
                turned_weights["low"] = turn_weights(w_low_rows, LOW_PASSES, "low")
            if step == 3:
                quantise_weights(turned_weights["low"], LOW_PASSES, "low")
            if step == W_HIGH_TURN:
                turned_weights["high"] = turn_weights(w_high_rows, HIGH_PASSES, "high")
            if step == W_HIGH_TURN + 2:
                quantise_weights(turned_weights["high"], HIGH_PASSES, "high")
            if 1 <= step <= len(chunks):
                quantise_chunk(chunks[step - 1])
            for task, subject in later.pop(step, []) if step < len(chunks) else ():
                task(subject)

        before, last = chunks[-2:]
        first_group, second_group, third_group = last["group"]["bank"]["groups"]
        other = chunks[-HALF_PAIRS - 1]["group"]
        low = banks[HALVES - 1]["groups"][0]
        for task, subject in (
            (square_pair, chunks[-3]),
            (sum_pair, chunks[-4]),
            (invert_norms, other),
            (invert_norms, low),
            (multiply_chunk, last),
            (square_pair, before),
            (sum_pair, chunks[-3]),
            (divide_by_norms, other),
            (divide_by_norms, low),
            (quantise_units, other),
            (square_pair, last),
            (sum_pair, before),
            (invert_norms, first_group),
            (divide_by_norms, first_group),
            (quantise_units, low),
            (sum_pair, last),
            (invert_norms, second_group),
            (divide_by_norms, second_group),
            (invert_norms, third_group),
            (divide_by_norms, third_group),
            (quantise_units, third_group),
        ):
            task(subject)

        link = turns.tile([NODES, NODES], F32, name="link", tag="turn")
        for half in range(HALVES):
            lo, hi = units["low_%d" % half], units["high_%d" % half]
            nc.tensor.matmul_mx(
                out=link[:],
                lhsT=lo[0][:].bitcast(FP8X4),
                lhsT_scale=lo[1][:],
                rhs=hi[0][:].bitcast(FP8X4),
                rhs_scale=hi[1][:],
                start=(half == 0),
                stop=(half == HALVES - 1),
            )
        result = keep.tile([NODES, NODES], F32)
        nc.scalar.mul(result[:], link[:], 1.0 / SAMPLES)
        nc.sync.dma_start(out=out, in_=result[:])
